import numpy as np
import ml_dtypes


def mxq(x, axis, fmt="e4m3"):
    dtype, down = {"e4m3": (ml_dtypes.float8_e4m3fn, 7), "e5m2": (ml_dtypes.float8_e5m2, 14)}[fmt]
    v = np.moveaxis(np.asarray(x, np.float32).astype(ml_dtypes.bfloat16).astype(np.float64), axis, -1)
    blocks = v.reshape(v.shape[:-1] + (-1, 32))
    amax = np.abs(blocks).max(-1, keepdims=True)
    byte = np.maximum(np.where(amax > 0, np.frexp(amax)[1] - 1 + 127, 0) - down, 1)
    scale = np.exp2(byte - 127.0)
    codes = (blocks / scale).astype(np.float32).astype(dtype).astype(np.float64)
    return np.moveaxis((codes * scale).reshape(v.shape), -1, axis)


WIDE = False


def mx_kscale(k):
    if not WIDE:
        return np.ones(k)
    levels = np.array([10, -10, 5, -5, 0])
    a = np.random.permutation(np.resize(levels, k // 512 * 4)).reshape(k // 512, 4)
    idx = np.arange(k)
    return np.exp2(a[idx // 512, idx % 128 // 32])


BF16 = ml_dtypes.bfloat16


def bf(x):
    return np.asarray(x, np.float32).astype(BF16)


def f64(x):
    return np.asarray(x).astype(np.float64)


B, S, D, K = 128, 8, 1024, 2048


def setup_inputs():
    t = np.exp2(np.round(np.log2(mx_kscale(D)) / 2))
    q = np.random.standard_normal((B, S, D))
    a = 0.3 * np.random.standard_normal((B, S, 1))
    p = np.random.standard_normal((B, S, D)) + a * q[:, -1:, :]
    W = np.random.uniform(0.0, 1.0, (K, D)) * np.sqrt(12.0 / D)
    return {"p": bf(p / t), "q": bf(q / t), "W": bf(W * t)}


def reference(p, q, W):
    p, q, W = f64(p), f64(q), f64(W)
    W2 = mxq(W * W, 1, "e4m3")
    q_last = q[:, -1, :]
    dot = (mxq(p * q_last[:, None, :], 2, "e4m3") @ W2.T).transpose(0, 2, 1)
    norm_p = np.sqrt((mxq(p * p, 2, "e4m3") @ W2.T).transpose(0, 2, 1))
    norm_q = np.sqrt(mxq(q_last * q_last, 1, "e4m3") @ W2.T)
    dist = -dot / (norm_p * norm_q[:, :, None] * D)
    return dist.reshape(B, S, -1)

@@ -1,0 +1,480 @@
+from contextlib import ExitStack
+
+import concourse.mybir as mybir
+from concourse.masks import make_identity
+
+F32 = mybir.dt.float32
+BF16 = mybir.dt.bfloat16
+U32 = mybir.dt.uint32
+U8 = mybir.dt.uint8
+FP8X4 = mybir.dt.float8_e4m3fn_x4
+ACT = mybir.ActivationFunctionType
+ALU = mybir.AluOpType
+
+P = 128
+B, S, D, K = 128, 8, 1024, 2048
+KC = 256
+NCH = K // KC
+NSP = S // 2
+PC = ["S","S","S","S"]
+WM = ["VV","SV","S","S","S","S","S","S"]
+LOADS = ["w0","p0","q","w1","p1","w2","w3","p2","p3","w4","w5","w6","w7"]
+SEQ = [
+    ("wT", 0),
+    ("wS", 0, 0),
+    ("pT", 0),
+    ("wT", 1),
+    ("wS", 0, 1),
+    ("pC", 0),
+    ("wQ", 0),
+    ("qT",),
+    ("pP", 0),
+    ("wS", 1, 0),
+    ("wS", 1, 1),
+    ("qS",),
+    ("qC",),
+    ("pQ", 0),
+    ("pT", 1),
+    ("pC", 1),
+    ("wQ", 1),
+    ("wT", 2),
+    ("wS", 2, 0),
+    ("qQ",),
+    ("nM", 1),
+    ("pR", 0),
+    ("uN", 1, 0),
+    ("wS", 2, 1),
+    ("wT", 3),
+    ("pP", 1),
+    ("nM", 0),
+    ("uN", 0, 0),
+    ("pU", 0),
+    ("uD", 0, 0),
+    ("nE", 1),
+    ("nE", 0),
+    ("wS", 3, 0),
+    ("pQ", 1),
+    ("pR", 1),
+    ("pT", 2),
+    ("uD", 1, 0),
+    ("pU", 1),
+    ("uN", 0, 1),
+    ("uR", 1, 0),
+    ("uN", 1, 1),
+    ("wQ", 2),
+    ("uD", 1, 1),
+    ("uR", 0, 0),
+    ("wS", 3, 1),
+    ("pT", 3),
+    ("uN", 2, 0),
+    ("uT", 0, 0),
+    ("uD", 0, 1),
+    ("pC", 2),
+    ("wQ", 3),
+    ("uT", 1, 0),
+    ("nM", 2),
+    ("uR", 0, 1),
+    ("uR", 1, 1),
+    ("uD", 2, 0),
+    ("pP", 2),
+    ("uR", 2, 0),
+    ("uT", 1, 1),
+    ("uT", 0, 1),
+    ("uT", 2, 0),
+    ("uN", 2, 1),
+    ("uN", 3, 0),
+    ("pC", 3),
+    ("uR", 3, 0),
+    ("pR", 2),
+    ("uD", 3, 0),
+    ("nE", 2),
+    ("wT", 4),
+    ("wS", 4, 0),
+    ("pQ", 2),
+    ("uR", 2, 1),
+    ("nM", 3),
+    ("pU", 2),
+    ("wS", 4, 1),
+    ("uT", 3, 0),
+    ("uD", 2, 1),
+    ("uT", 2, 1),
+    ("wT", 5),
+    ("pP", 3),
+    ("uN", 3, 1),
+    ("nE", 3),
+    ("uR", 3, 1),
+    ("uN", 1, 2),
+    ("uR", 1, 2),
+    ("uD", 3, 1),
+    ("uT", 3, 1),
+    ("wS", 5, 0),
+    ("uN", 0, 2),
+    ("uR", 0, 2),
+    ("uN", 2, 2),
+    ("uD", 2, 2),
+    ("pR", 3),
+    ("pQ", 3),
+    ("uD", 0, 2),
+    ("uR", 2, 2),
+    ("uD", 1, 2),
+    ("wT", 6),
+    ("uN", 3, 2),
+    ("uT", 1, 2),
+    ("wS", 5, 1),
+    ("uN", 3, 3),
+    ("uN", 0, 3),
+    ("uT", 2, 2),
+    ("uT", 0, 2),
+    ("uD", 3, 2),
+    ("uR", 3, 2),
+    ("pU", 3),
+    ("uD", 3, 3),
+    ("wQ", 4),
+    ("uR", 3, 3),
+    ("uN", 1, 3),
+    ("uN", 4, 2),
+    ("uT", 3, 2),
+    ("uD", 0, 3),
+    ("uT", 3, 3),
+    ("uR", 0, 3),
+    ("wQ", 5),
+    ("uN", 2, 3),
+    ("uT", 0, 3),
+    ("uR", 1, 3),
+    ("thV", 0, 0, 128),
+    ("nM", 4),
+    ("uR", 4, 2),
+    ("uD", 1, 3),
+    ("uN", 4, 0),
+    ("uT", 1, 3),
+    ("uD", 4, 2),
+    ("uT", 4, 2),
+    ("thG", 3, 64, 256),
+    ("uN", 4, 1),
+    ("uR", 2, 3),
+    ("thV", 3, 0, 64),
+    ("nE", 4),
+    ("uD", 2, 3),
+    ("wS", 6, 0),
+    ("uD", 4, 0),
+    ("nM", 5),
+    ("uR", 4, 0),
+    ("wS", 6, 1),
+    ("wT", 7),
+    ("uN", 5, 1),
+    ("nE", 5),
+    ("uN", 4, 3),
+    ("uR", 4, 1),
+    ("uT", 2, 3),
+    ("uD", 4, 1),
+    ("wQ", 6),
+    ("thG", 0, 128, 256),
+    ("uN", 5, 3),
+    ("wS", 7, 0),
+    ("thG", 1, 128, 256),
+    ("uT", 4, 0),
+    ("uD", 5, 1),
+    ("uR", 5, 1),
+    ("thV", 2, 0, 96),
+    ("uT", 4, 1),
+    ("uR", 4, 3),
+    ("uT", 5, 1),
+    ("uR", 5, 3),
+    ("uD", 4, 3),
+    ("nM", 6),
+    ("uN", 5, 0),
+    ("uN", 5, 2),
+    ("uD", 5, 0),
+    ("uD", 5, 3),
+    ("uN", 6, 0),
+    ("uT", 4, 3),
+    ("thV", 1, 0, 128),
+    ("uD", 5, 2),
+    ("uD", 6, 0),
+    ("thG", 2, 96, 256),
+    ("nE", 6),
+    ("uN", 6, 3),
+    ("wS", 7, 1),
+    ("uR", 5, 0),
+    ("uR", 5, 2),
+    ("wQ", 7),
+    ("nM", 7),
+    ("uD", 6, 3),
+    ("uN", 6, 1),
+    ("uN", 6, 2),
+    ("uD", 6, 2),
+    ("uT", 5, 3),
+    ("uD", 6, 1),
+    ("uN", 7, 3),
+    ("uR", 6, 0),
+    ("uR", 6, 3),
+    ("thG", 4, 64, 256),
+    ("uT", 5, 0),
+    ("uN", 7, 0),
+    ("uT", 5, 2),
+    ("uD", 7, 3),
+    ("thV", 4, 0, 64),
+    ("nE", 7),
+    ("uD", 7, 0),
+    ("uT", 6, 0),
+    ("uR", 6, 2),
+    ("uR", 6, 1),
+    ("uT", 6, 3),
+    ("uR", 7, 3),
+    ("uN", 7, 1),
+    ("uT", 6, 2),
+    ("uT", 6, 1),
+    ("uR", 7, 0),
+    ("thV", 6, 0, 96),
+    ("thV", 5, 0, 32),
+    ("uT", 7, 0),
+    ("thG", 5, 32, 256),
+    ("uN", 7, 2),
+    ("uR", 7, 1),
+    ("uT", 7, 3),
+    ("uD", 7, 1),
+    ("uD", 7, 2),
+    ("uR", 7, 2),
+    ("uT", 7, 1),
+    ("uT", 7, 2),
+    ("thG", 6, 96, 256),
+    ("thG", 7, 192, 256),
+    ("thV", 7, 0, 192),
+]
+
+FLOPS = 2 * (2 * B * S + B) * K * D
+
+
+def tile_mpl_kernel(tc, p, q, W, out):
+    nc = tc.nc
+    out_flat = out.rearrange("b s k -> b (s k)")
+    with ExitStack() as ctx:
+        const = ctx.enter_context(tc.tile_pool(name="const", bufs=1))
+        keep = ctx.enter_context(tc.tile_pool(name="keep", bufs=1))
+        grp = ctx.enter_context(tc.tile_pool(name="grp", bufs=2))
+        epi = ctx.enter_context(tc.tile_pool(name="epi", bufs=3))
+        tpool = ctx.enter_context(tc.tile_pool(name="tpool", bufs=5))
+        ps_tp = ctx.enter_context(tc.psum_pool(name="ps_tp", bufs=3))
+        ps_mx = ctx.enter_context(tc.psum_pool(name="ps_mx", bufs=5))
+        ctx.enter_context(tc.manual_schedule())
+
+        q_sb = const.tile([P, D], BF16, name="q_sb")
+        p_sb = [const.tile([P, 2, D], BF16, name="p_sb%d" % sp) for sp in range(NSP)]
+        w_sb = [const.tile([P, 2, D], BF16, name="w_sb%d" % c) for c in range(NCH)]
+        for name in LOADS:
+            i = int(name[1:]) if len(name) > 1 else 0
+            if name[0] == "q":
+                nc.sync.dma_start(out=q_sb[:], in_=q[:, S - 1, :])
+            elif name[0] == "p":
+                nc.sync.dma_start(out=p_sb[i][:], in_=p[:, 2 * i : 2 * i + 2, :])
+            else:
+                nc.sync.dma_start(
+                    out=w_sb[i][:], in_=W[KC * i : KC * (i + 1), :].rearrange("(t r) d -> r t d", r=P)
+                )
+
+        ident = const.tile([P, P], F32, name="ident")
+        make_identity(nc, ident[:])
+        one = const.tile([P, 1], F32, name="one")
+        nc.vector.memset(one[:], 1.0)
+        warm = const.tile([P, 1], F32, name="warm")
+        nc.scalar.activation(out=warm[:], in_=one[:], func=ACT.Abs_reciprocal_sqrt)
+
+        qg = const.tile([P, 2, 512], BF16, name="qg")
+        gq = const.tile([P, 1024], BF16, name="gq", align_bytes=64)
+        qc = keep.tile([P, 256], U32, name="qc", align_bytes=64)
+        qs = keep.tile([P, 256], U8, name="qs", align_bytes=64)
+        pqc = [keep.tile([P, 512], U32, name="pqc%d" % sp, align_bytes=64) for sp in range(NSP)]
+        pqs = [keep.tile([P, 512], U8, name="pqs%d" % sp, align_bytes=64) for sp in range(NSP)]
+        ppc = [keep.tile([P, 512], U32, name="ppc%d" % sp, align_bytes=64) for sp in range(NSP)]
+        pps = [keep.tile([P, 512], U8, name="pps%d" % sp, align_bytes=64) for sp in range(NSP)]
+        wc = [keep.tile([P, 512], U32, name="wc%d" % c, align_bytes=64) for c in range(NCH)]
+        ws = [keep.tile([P, 512], U8, name="ws%d" % c, align_bytes=64) for c in range(NCH)]
+        T = {}
+
+        def transposes(bank, rows, g):
+            for u in range(2):
+                for t in range(2):
+                    nc.tensor.transpose(
+                        out=bank[:, u * 256 + t * P : u * 256 + (t + 1) * P],
+                        in_=rows[:, t, :].bitcast(F32)[:, 256 * g + P * u : 256 * g + P * (u + 1)],
+                        identity=ident[:],
+                    )
+
+        def words_out(eng, dst, bank):
+            src = bank[:].rearrange("p (u n) -> p n u", u=2)
+            dstw = dst.bitcast(F32).rearrange("p (n u) -> p n u", u=2)
+            if eng == "S":
+                nc.scalar.copy(out=dstw, in_=src)
+            else:
+                nc.vector.tensor_copy(out=dstw, in_=src)
+
+        def square_out(dst, bank):
+            nc.scalar.activation(
+                out=dst.rearrange("p (n u e) -> p n u e", u=2, e=2),
+                in_=bank[:].bitcast(BF16).rearrange("p (u n e) -> p n u e", u=2, e=2),
+                func=ACT.Square,
+            )
+
+        def quant(codes, scales, src):
+            nc.vector.quantize_mx(out=codes[:].bitcast(FP8X4), scales=scales[:], in_=src)
+
+        def qT():
+            bank = ps_tp.tile([P, 512], F32, name="tb", tag="tb")
+            T["qb"] = bank
+            for u in range(2):
+                for g in range(2):
+                    nc.tensor.transpose(
+                        out=bank[:, u * 256 + g * P : u * 256 + (g + 1) * P],
+                        in_=q_sb[:].bitcast(F32)[:, 256 * g + P * u : 256 * g + P * (u + 1)],
+                        identity=ident[:],
+                    )
+
+        def qC():
+            words_out("S", qg[:].rearrange("p g n -> p (g n)"), T["qb"])
+
+        def qS():
+            square_out(gq[:], T["qb"])
+
+        def qQ():
+            quant(qc, qs, gq[:])
+
+        def pT(sp):
+            for g in range(2):
+                bank = ps_tp.tile([P, 512], F32, name="tb", tag="tb")
+                T["pb", sp, g] = bank
+                transposes(bank, p_sb[sp], g)
+
+        def pC(sp):
+            pt = grp.tile([P, 2, 1024], BF16, name="pt")
+            T["pt", sp] = pt
+            for g in range(2):
+                words_out(PC[sp], pt[:, g, :], T["pb", sp, g])
+
+        def pP(sp):
+            gpp = grp.tile([P, 2048], BF16, name="gpp", align_bytes=64)
+            T["gpp", sp] = gpp
+            flat = T["pt", sp][:].rearrange("p g n -> p (g n)")
+            nc.vector.tensor_tensor(out=gpp[:], in0=flat, in1=flat, op=ALU.mult)
+
+        def pR(sp):
+            gpq = grp.tile([P, 2, 1024], BF16, name="gpq", align_bytes=64)
+            T["gpq", sp] = gpq
+            for g in range(2):
+                nc.vector.tensor_tensor(
+                    out=gpq[:, g, :].rearrange("p (s n) -> p s n", s=2),
+                    in0=T["pt", sp][:, g, :].rearrange("p (s n) -> p s n", s=2),
+                    in1=qg[:, g, :].unsqueeze(1).to_broadcast([P, 2, 512]),
+                    op=ALU.mult,
+                )
+
+        def pQ(sp):
+            quant(ppc[sp], pps[sp], T["gpp", sp][:])
+
+        def pU(sp):
+            quant(pqc[sp], pqs[sp], T["gpq", sp][:].rearrange("p g n -> p (g n)"))
+
+        def wT(c):
+            for g in range(2):
+                bank = ps_tp.tile([P, 512], F32, name="tb", tag="tb")
+                T["wb", c, g] = bank
+                transposes(bank, w_sb[c], g)
+
+        def wS(c, g):
+            if g == 0:
+                T["gw", c] = grp.tile([P, 2, 1024], BF16, name="gw", align_bytes=64)
+            gw = T["gw", c]
+            if WM[c] == "S":
+                square_out(gw[:, g, :], T["wb", c, g])
+            else:
+                wt = grp.tile([P, 1024], BF16, name="wt")
+                words_out(WM[c][0], wt[:], T["wb", c, g])
+                nc.vector.tensor_tensor(out=gw[:, g, :], in0=wt[:], in1=wt[:], op=ALU.mult)
+
+        def wQ(c):
+            quant(wc[c], ws[c], T["gw", c][:].rearrange("p g n -> p (g n)"))
+
+        def group(dst, lc, ls, first, c):
+            for g in range(2):
+                col = (first + 2 * g) * P if first >= 0 else g * P
+                nc.tensor.matmul_mx(
+                    out=dst,
+                    lhsT=lc[:, col : col + P].bitcast(FP8X4),
+                    lhsT_scale=ls[:, col : col + P],
+                    rhs=wc[c][:, g * KC : (g + 1) * KC].bitcast(FP8X4),
+                    rhs_scale=ws[c][:, g * KC : (g + 1) * KC],
+                    start=(g == 0),
+                    stop=(g == 1),
+                )
+
+        def nM(c):
+            bank = ps_mx.tile([P, 512], F32, name="mb", tag="mb")
+            T["nq", c] = bank
+            group(bank[:, 0:KC], qc, qs, -1, c)
+
+        def nE(c):
+            rq = keep.tile([P, KC], F32, name="rq%d" % c)
+            T["rq", c] = rq
+            nc.scalar.activation(
+                out=rq[:], in_=T["nq", c][:, 0:KC], func=ACT.Abs_reciprocal_sqrt, scale=float(D * D)
+            )
+
+        def uN(c, sp):
+            bank = ps_mx.tile([P, 512], F32, name="mb", tag="mb")
+            T["nb", c, sp] = bank
+            for s in range(2):
+                group(bank[:, s * KC : (s + 1) * KC], ppc[sp], pps[sp], s, c)
+
+        def uD(c, sp):
+            bank = ps_mx.tile([P, 512], F32, name="mb", tag="mb")
+            T["db", c, sp] = bank
+            for s in range(2):
+                group(bank[:, s * KC : (s + 1) * KC], pqc[sp], pqs[sp], s, c)
+
+        def uR(c, sp):
+            r = epi.tile([P, 2 * KC], F32, name="r")
+            T["r", c, sp] = r
+            nc.scalar.activation(
+                out=r[:].rearrange("p (k s) -> p k s", s=2),
+                in_=T["nb", c, sp][:].rearrange("p (s k) -> p k s", s=2),
+                func=ACT.Abs_reciprocal_sqrt,
+            )
+
+        def uT(c, sp):
+            if ("tt", c) not in T:
+                T["tt", c] = tpool.tile([P, NSP, 2 * KC], F32, name="tt")
+            nc.vector.scalar_tensor_tensor(
+                out=T["tt", c][:, sp, :].rearrange("p (k s) -> p k s", s=2),
+                in0=T["db", c, sp][:].rearrange("p (s k) -> p k s", s=2),
+                scalar=-1.0,
+                in1=T["r", c, sp][:].rearrange("p (k s) -> p k s", s=2),
+                op0=ALU.mult,
+                op1=ALU.mult,
+            )
+
+        def third(eng, o, c, lo, hi):
+            eng.tensor_tensor(
+                out=o[:, 0 : (hi - lo) * S].rearrange("p (k a s) -> p k a s", a=NSP, s=2),
+                in0=T["tt", c][:].rearrange("p a (k s) -> p k a s", s=2)[:, lo:hi, :, :],
+                in1=T["rq", c][:, lo:hi].unsqueeze(2).unsqueeze(3).to_broadcast([P, hi - lo, NSP, 2]),
+                op=ALU.mult,
+            )
+            nc.sync.dma_start(
+                out=out_flat[:, (c * KC + lo) * S : (c * KC + hi) * S], in_=o[:, 0 : (hi - lo) * S]
+            )
+
+        def thV(c, lo, hi):
+            ov = epi.tile([P, 192 * S], F32, name="ov")
+            third(nc.vector, ov, c, lo, hi)
+
+        def thG(c, lo, hi):
+            og = epi.tile([P, 224 * S], F32, name="og")
+            third(nc.gpsimd, og, c, lo, hi)
+
+        steps = {
+            "qT": qT, "qC": qC, "qS": qS, "qQ": qQ,
+            "pT": pT, "pC": pC, "pP": pP, "pR": pR, "pQ": pQ, "pU": pU,
+            "wT": wT, "wS": wS, "wQ": wQ, "nM": nM, "nE": nE,
+            "uN": uN, "uD": uD, "uR": uR, "uT": uT, "thV": thV, "thG": thG,
+        }
+        for step in SEQ:
+            steps[step[0]](*step[1:])

@@ -21,225 +21,223 @@ WM = ["VV","SV","S","S","S","S","S","S"]
 LOADS = ["w0","p0","q","w1","p1","w2","w3","p2","p3","w4","w5","w6","w7"]
 SEQ = [
     ("wT", 0),
-    ("wS", 0, 0),
     ("pT", 0),
+    ("qT",),
+    ("wS", 0, 0),
+    ("pC", 0),
     ("wT", 1),
     ("wS", 0, 1),
-    ("pC", 0),
-    ("wQ", 0),
-    ("qT",),
     ("pP", 0),
-    ("wS", 1, 0),
-    ("wS", 1, 1),
-    ("qS",),
-    ("qC",),
     ("pQ", 0),
+    ("qC",),
+    ("wS", 1, 0),
+    ("wQ", 0),
+    ("qS",),
     ("pT", 1),
+    ("wS", 1, 1),
     ("pC", 1),
     ("wQ", 1),
-    ("wT", 2),
-    ("wS", 2, 0),
     ("qQ",),
-    ("nM", 1),
     ("pR", 0),
+    ("wT", 2),
+    ("pP", 1),
+    ("pU", 0),
+    ("nM", 1),
+    ("pQ", 1),
+    ("wT", 3),
+    ("pR", 1),
+    ("uN", 0, 0),
+    ("wS", 2, 0),
     ("uN", 1, 0),
     ("wS", 2, 1),
-    ("wT", 3),
-    ("pP", 1),
-    ("nM", 0),
-    ("uN", 0, 0),
-    ("pU", 0),
-    ("uD", 0, 0),
-    ("nE", 1),
-    ("nE", 0),
     ("wS", 3, 0),
-    ("pQ", 1),
-    ("pR", 1),
-    ("pT", 2),
-    ("uD", 1, 0),
+    ("nE", 1),
     ("pU", 1),
-    ("uN", 0, 1),
-    ("uR", 1, 0),
+    ("uD", 0, 0),
     ("uN", 1, 1),
+    ("uN", 0, 1),
+    ("uR", 0, 0),
+    ("pT", 2),
+    ("wS", 3, 1),
     ("wQ", 2),
     ("uD", 1, 1),
-    ("uR", 0, 0),
-    ("wS", 3, 1),
-    ("pT", 3),
-    ("uN", 2, 0),
     ("uT", 0, 0),
-    ("uD", 0, 1),
-    ("pC", 2),
     ("wQ", 3),
-    ("uT", 1, 0),
-    ("nM", 2),
-    ("uR", 0, 1),
-    ("uR", 1, 1),
+    ("uD", 0, 1),
+    ("uD", 1, 0),
     ("uD", 2, 0),
-    ("pP", 2),
+    ("uR", 1, 0),
+    ("uR", 1, 1),
+    ("uR", 0, 1),
+    ("pC", 2),
+    ("uN", 2, 0),
     ("uR", 2, 0),
+    ("pT", 3),
     ("uT", 1, 1),
-    ("uT", 0, 1),
-    ("uT", 2, 0),
-    ("uN", 2, 1),
-    ("uN", 3, 0),
-    ("pC", 3),
-    ("uR", 3, 0),
-    ("pR", 2),
-    ("uD", 3, 0),
-    ("nE", 2),
-    ("wT", 4),
-    ("wS", 4, 0),
-    ("pQ", 2),
-    ("uR", 2, 1),
     ("nM", 3),
-    ("pU", 2),
-    ("wS", 4, 1),
-    ("uT", 3, 0),
-    ("uD", 2, 1),
-    ("uT", 2, 1),
-    ("wT", 5),
-    ("pP", 3),
+    ("uT", 1, 0),
+    ("uT", 0, 1),
+    ("pC", 3),
+    ("wT", 4),
+    ("uN", 2, 1),
     ("uN", 3, 1),
-    ("nE", 3),
-    ("uR", 3, 1),
-    ("uN", 1, 2),
-    ("uR", 1, 2),
+    ("uN", 3, 0),
+    ("pP", 2),
+    ("uT", 2, 0),
     ("uD", 3, 1),
-    ("uT", 3, 1),
-    ("wS", 5, 0),
+    ("wS", 4, 0),
+    ("nM", 0),
+    ("uR", 2, 1),
+    ("uD", 3, 0),
+    ("wT", 5),
+    ("nE", 3),
+    ("pQ", 2),
+    ("pR", 2),
+    ("uR", 3, 0),
+    ("uD", 2, 1),
+    ("uN", 1, 2),
+    ("nM", 2),
     ("uN", 0, 2),
-    ("uR", 0, 2),
-    ("uN", 2, 2),
-    ("uD", 2, 2),
+    ("uR", 3, 1),
+    ("wS", 4, 1),
     ("pR", 3),
-    ("pQ", 3),
-    ("uD", 0, 2),
-    ("uR", 2, 2),
-    ("uD", 1, 2),
-    ("wT", 6),
+    ("uN", 2, 2),
+    ("pP", 3),
+    ("uT", 3, 1),
+    ("nE", 0),
+    ("wS", 5, 0),
+    ("uT", 3, 0),
+    ("uT", 2, 1),
+    ("pU", 2),
     ("uN", 3, 2),
-    ("uT", 1, 2),
+    ("uD", 1, 2),
+    ("nE", 2),
+    ("uR", 1, 2),
+    ("uD", 0, 2),
+    ("pQ", 3),
+    ("wT", 6),
+    ("pU", 3),
     ("wS", 5, 1),
     ("uN", 3, 3),
-    ("uN", 0, 3),
-    ("uT", 2, 2),
-    ("uT", 0, 2),
+    ("uR", 0, 2),
+    ("uR", 2, 2),
     ("uD", 3, 2),
     ("uR", 3, 2),
-    ("pU", 3),
-    ("uD", 3, 3),
     ("wQ", 4),
-    ("uR", 3, 3),
-    ("uN", 1, 3),
-    ("uN", 4, 2),
-    ("uT", 3, 2),
+    ("uD", 3, 3),
+    ("uT", 1, 2),
     ("uD", 0, 3),
-    ("uT", 3, 3),
-    ("uR", 0, 3),
-    ("wQ", 5),
+    ("uD", 2, 2),
+    ("uR", 3, 3),
+    ("uN", 0, 3),
     ("uN", 2, 3),
-    ("uT", 0, 3),
-    ("uR", 1, 3),
-    ("thV", 0, 0, 128),
-    ("nM", 4),
-    ("uR", 4, 2),
-    ("uD", 1, 3),
-    ("uN", 4, 0),
-    ("uT", 1, 3),
-    ("uD", 4, 2),
-    ("uT", 4, 2),
-    ("thG", 3, 64, 256),
-    ("uN", 4, 1),
-    ("uR", 2, 3),
-    ("thV", 3, 0, 64),
-    ("nE", 4),
-    ("uD", 2, 3),
+    ("uT", 0, 2),
+    ("uR", 0, 3),
     ("wS", 6, 0),
-    ("uD", 4, 0),
-    ("nM", 5),
-    ("uR", 4, 0),
+    ("wQ", 5),
+    ("uN", 1, 3),
+    ("uT", 3, 2),
+    ("uT", 3, 3),
+    ("uD", 2, 3),
+    ("uT", 2, 2),
+    ("uR", 2, 3),
+    ("uD", 1, 3),
+    ("uR", 1, 3),
     ("wS", 6, 1),
     ("wT", 7),
-    ("uN", 5, 1),
-    ("nE", 5),
+    ("uT", 0, 3),
+    ("nM", 4),
+    ("uN", 4, 2),
     ("uN", 4, 3),
-    ("uR", 4, 1),
+    ("thV", 0, 0, 224),
+    ("nE", 4),
     ("uT", 2, 3),
-    ("uD", 4, 1),
-    ("wQ", 6),
-    ("thG", 0, 128, 256),
-    ("uN", 5, 3),
-    ("wS", 7, 0),
-    ("thG", 1, 128, 256),
-    ("uT", 4, 0),
+    ("uN", 4, 0),
+    ("uD", 4, 2),
+    ("uR", 4, 2),
+    ("uD", 4, 0),
     ("uD", 5, 1),
-    ("uR", 5, 1),
-    ("thV", 2, 0, 96),
-    ("uT", 4, 1),
-    ("uR", 4, 3),
-    ("uT", 5, 1),
-    ("uR", 5, 3),
+    ("uT", 1, 3),
+    ("uR", 4, 0),
+    ("uT", 4, 0),
+    ("uT", 4, 2),
+    ("uN", 5, 1),
     ("uD", 4, 3),
-    ("nM", 6),
-    ("uN", 5, 0),
+    ("wQ", 6),
+    ("thG", 3, 128, 256),
+    ("uN", 4, 1),
+    ("uR", 4, 3),
+    ("uD", 4, 1),
     ("uN", 5, 2),
-    ("uD", 5, 0),
-    ("uD", 5, 3),
-    ("uN", 6, 0),
+    ("uR", 5, 1),
+    ("thG", 0, 224, 256),
+    ("uN", 5, 3),
+    ("nM", 5),
+    ("uN", 5, 0),
+    ("uT", 5, 1),
     ("uT", 4, 3),
-    ("thV", 1, 0, 128),
+    ("uR", 4, 1),
+    ("wS", 7, 0),
+    ("uT", 4, 1),
     ("uD", 5, 2),
-    ("uD", 6, 0),
-    ("thG", 2, 96, 256),
-    ("nE", 6),
-    ("uN", 6, 3),
-    ("wS", 7, 1),
+    ("nM", 6),
     ("uR", 5, 0),
+    ("uD", 5, 3),
+    ("uD", 5, 0),
+    ("uN", 6, 3),
+    ("thV", 1, 0, 160),
+    ("uN", 6, 0),
     ("uR", 5, 2),
+    ("thG", 2, 64, 256),
+    ("thV", 4, 0, 256),
+    ("uN", 6, 1),
+    ("uD", 6, 0),
+    ("wS", 7, 1),
     ("wQ", 7),
+    ("nE", 6),
     ("nM", 7),
     ("uD", 6, 3),
-    ("uN", 6, 1),
-    ("uN", 6, 2),
-    ("uD", 6, 2),
-    ("uT", 5, 3),
-    ("uD", 6, 1),
-    ("uN", 7, 3),
+    ("thV", 3, 0, 128),
+    ("nE", 5),
+    ("uR", 5, 3),
     ("uR", 6, 0),
     ("uR", 6, 3),
-    ("thG", 4, 64, 256),
-    ("uT", 5, 0),
-    ("uN", 7, 0),
-    ("uT", 5, 2),
-    ("uD", 7, 3),
-    ("thV", 4, 0, 64),
+    ("uD", 6, 1),
     ("nE", 7),
-    ("uD", 7, 0),
-    ("uT", 6, 0),
-    ("uR", 6, 2),
     ("uR", 6, 1),
-    ("uT", 6, 3),
-    ("uR", 7, 3),
-    ("uN", 7, 1),
-    ("uT", 6, 2),
+    ("uT", 5, 2),
+    ("uN", 7, 3),
+    ("uT", 5, 0),
+    ("thG", 1, 160, 256),
+    ("uN", 6, 2),
+    ("uN", 7, 0),
+    ("uT", 5, 3),
+    ("uR", 6, 2),
+    ("uD", 6, 2),
+    ("uD", 7, 3),
+    ("thV", 2, 0, 64),
+    ("uT", 6, 0),
     ("uT", 6, 1),
-    ("uR", 7, 0),
-    ("thV", 6, 0, 96),
-    ("thV", 5, 0, 32),
-    ("uT", 7, 0),
-    ("thG", 5, 32, 256),
+    ("uT", 6, 3),
     ("uN", 7, 2),
-    ("uR", 7, 1),
+    ("uN", 7, 1),
+    ("uR", 7, 3),
+    ("uD", 7, 0),
+    ("thG", 5, 0, 256),
+    ("uT", 6, 2),
+    ("thV", 6, 0, 128),
+    ("uR", 7, 0),
     ("uT", 7, 3),
+    ("uR", 7, 1),
     ("uD", 7, 1),
-    ("uD", 7, 2),
     ("uR", 7, 2),
+    ("uT", 7, 0),
+    ("uD", 7, 2),
     ("uT", 7, 1),
     ("uT", 7, 2),
-    ("thG", 6, 96, 256),
-    ("thG", 7, 192, 256),
+    ("thG", 6, 128, 256),
     ("thV", 7, 0, 192),
+    ("thG", 7, 192, 256),
 ]
 
 FLOPS = 2 * (2 * B * S + B) * K * D
@@ -463,11 +461,11 @@ def tile_mpl_kernel(tc, p, q, W, out):
             )
 
         def thV(c, lo, hi):
-            ov = epi.tile([P, 192 * S], F32, name="ov")
+            ov = epi.tile([P, 256 * S], F32, name="ov")
             third(nc.vector, ov, c, lo, hi)
 
         def thG(c, lo, hi):
-            og = epi.tile([P, 224 * S], F32, name="og")
+            og = epi.tile([P, 256 * S], F32, name="og")
             third(nc.gpsimd, og, c, lo, hi)
 
         steps = {

@@ -17,227 +17,229 @@ KC = 256
 NCH = K // KC
 NSP = S // 2
 PC = ["S","S","S","S"]
-WM = ["VV","SV","S","S","S","S","S","S"]
+WM = ["SV","S","S","S","S","S","S","S"]
 LOADS = ["w0","p0","q","w1","p1","w2","w3","p2","p3","w4","w5","w6","w7"]
 SEQ = [
     ("wT", 0),
     ("pT", 0),
     ("qT",),
     ("wS", 0, 0),
-    ("pC", 0),
-    ("wT", 1),
     ("wS", 0, 1),
-    ("pP", 0),
-    ("pQ", 0),
+    ("pC", 0),
     ("qC",),
-    ("wS", 1, 0),
-    ("wQ", 0),
     ("qS",),
     ("pT", 1),
-    ("wS", 1, 1),
-    ("pC", 1),
-    ("wQ", 1),
-    ("qQ",),
+    ("wQ", 0),
+    ("pP", 0),
     ("pR", 0),
-    ("wT", 2),
+    ("pQ", 0),
+    ("qQ",),
+    ("pC", 1),
+    ("wT", 1),
+    ("wS", 1, 0),
+    ("wS", 1, 1),
     ("pP", 1),
-    ("pU", 0),
-    ("nM", 1),
-    ("pQ", 1),
-    ("wT", 3),
     ("pR", 1),
-    ("uN", 0, 0),
-    ("wS", 2, 0),
-    ("uN", 1, 0),
-    ("wS", 2, 1),
-    ("wS", 3, 0),
-    ("nE", 1),
+    ("pU", 0),
     ("pU", 1),
-    ("uD", 0, 0),
-    ("uN", 1, 1),
-    ("uN", 0, 1),
-    ("uR", 0, 0),
+    ("wQ", 1),
     ("pT", 2),
-    ("wS", 3, 1),
-    ("wQ", 2),
-    ("uD", 1, 1),
-    ("uT", 0, 0),
-    ("wQ", 3),
-    ("uD", 0, 1),
-    ("uD", 1, 0),
-    ("uD", 2, 0),
-    ("uR", 1, 0),
-    ("uR", 1, 1),
-    ("uR", 0, 1),
     ("pC", 2),
-    ("uN", 2, 0),
-    ("uR", 2, 0),
+    ("wT", 2),
+    ("wS", 2, 0),
     ("pT", 3),
-    ("uT", 1, 1),
-    ("nM", 3),
-    ("uT", 1, 0),
-    ("uT", 0, 1),
     ("pC", 3),
-    ("wT", 4),
-    ("uN", 2, 1),
-    ("uN", 3, 1),
-    ("uN", 3, 0),
     ("pP", 2),
-    ("uT", 2, 0),
-    ("uD", 3, 1),
-    ("wS", 4, 0),
-    ("nM", 0),
-    ("uR", 2, 1),
-    ("uD", 3, 0),
-    ("wT", 5),
-    ("nE", 3),
-    ("pQ", 2),
     ("pR", 2),
-    ("uR", 3, 0),
-    ("uD", 2, 1),
-    ("uN", 1, 2),
-    ("nM", 2),
-    ("uN", 0, 2),
-    ("uR", 3, 1),
-    ("wS", 4, 1),
-    ("pR", 3),
-    ("uN", 2, 2),
+    ("pQ", 2),
+    ("pQ", 1),
     ("pP", 3),
-    ("uT", 3, 1),
+    ("pR", 3),
+    ("nM", 0),
+    ("nM", 1),
     ("nE", 0),
-    ("wS", 5, 0),
-    ("uT", 3, 0),
-    ("uT", 2, 1),
+    ("nE", 1),
+    ("uN", 0, 0),
+    ("uD", 0, 0),
+    ("uR", 0, 0),
+    ("wS", 2, 1),
+    ("uN", 1, 0),
+    ("uD", 1, 0),
+    ("uR", 1, 0),
+    ("uT", 0, 0),
     ("pU", 2),
-    ("uN", 3, 2),
-    ("uD", 1, 2),
-    ("nE", 2),
-    ("uR", 1, 2),
-    ("uD", 0, 2),
-    ("pQ", 3),
-    ("wT", 6),
+    ("uT", 1, 0),
     ("pU", 3),
-    ("wS", 5, 1),
-    ("uN", 3, 3),
+    ("uN", 0, 1),
+    ("uD", 0, 1),
+    ("wT", 3),
+    ("wS", 3, 0),
+    ("uR", 0, 1),
+    ("uN", 1, 1),
+    ("uD", 1, 1),
+    ("uR", 1, 1),
+    ("uT", 0, 1),
+    ("uT", 1, 1),
+    ("pQ", 3),
+    ("wQ", 2),
+    ("uN", 0, 2),
+    ("uD", 0, 2),
     ("uR", 0, 2),
-    ("uR", 2, 2),
-    ("uD", 3, 2),
-    ("uR", 3, 2),
-    ("wQ", 4),
-    ("uD", 3, 3),
-    ("uT", 1, 2),
-    ("uD", 0, 3),
-    ("uD", 2, 2),
-    ("uR", 3, 3),
-    ("uN", 0, 3),
-    ("uN", 2, 3),
+    ("wS", 3, 1),
+    ("uN", 1, 2),
+    ("uD", 1, 2),
+    ("uR", 1, 2),
     ("uT", 0, 2),
+    ("uT", 1, 2),
+    ("uN", 0, 3),
+    ("uD", 0, 3),
     ("uR", 0, 3),
-    ("wS", 6, 0),
-    ("wQ", 5),
+    ("uT", 0, 3),
+    ("thV", 0, 0, 192),
+    ("thG", 0, 192, 256),
     ("uN", 1, 3),
-    ("uT", 3, 2),
-    ("uT", 3, 3),
-    ("uD", 2, 3),
-    ("uT", 2, 2),
-    ("uR", 2, 3),
     ("uD", 1, 3),
     ("uR", 1, 3),
-    ("wS", 6, 1),
-    ("wT", 7),
-    ("uT", 0, 3),
-    ("nM", 4),
-    ("uN", 4, 2),
-    ("uN", 4, 3),
-    ("thV", 0, 0, 224),
-    ("nE", 4),
-    ("uT", 2, 3),
-    ("uN", 4, 0),
-    ("uD", 4, 2),
-    ("uR", 4, 2),
-    ("uD", 4, 0),
-    ("uD", 5, 1),
     ("uT", 1, 3),
+    ("uN", 2, 0),
+    ("uD", 2, 0),
+    ("uR", 2, 0),
+    ("uN", 2, 1),
+    ("uD", 2, 1),
+    ("uR", 2, 1),
+    ("uT", 2, 0),
+    ("uT", 2, 1),
+    ("wQ", 3),
+    ("thV", 1, 0, 192),
+    ("thG", 1, 192, 256),
+    ("nM", 2),
+    ("nE", 2),
+    ("uN", 2, 2),
+    ("uD", 2, 2),
+    ("uR", 2, 2),
+    ("uT", 2, 2),
+    ("uN", 2, 3),
+    ("uD", 2, 3),
+    ("uR", 2, 3),
+    ("uT", 2, 3),
+    ("thV", 2, 0, 96),
+    ("thG", 2, 96, 256),
+    ("wT", 4),
+    ("uN", 3, 0),
+    ("uD", 3, 0),
+    ("wS", 4, 0),
+    ("uR", 3, 0),
+    ("uN", 3, 1),
+    ("uD", 3, 1),
+    ("uR", 3, 1),
+    ("uT", 3, 0),
+    ("uT", 3, 1),
+    ("nM", 3),
+    ("wS", 4, 1),
+    ("nE", 3),
+    ("uN", 3, 2),
+    ("uD", 3, 2),
+    ("wQ", 4),
+    ("uR", 3, 2),
+    ("uT", 3, 2),
+    ("uN", 3, 3),
+    ("uD", 3, 3),
+    ("uR", 3, 3),
+    ("uT", 3, 3),
+    ("thV", 3, 0, 96),
+    ("thG", 3, 96, 256),
+    ("wT", 5),
+    ("uN", 4, 0),
+    ("uD", 4, 0),
+    ("wS", 5, 0),
     ("uR", 4, 0),
-    ("uT", 4, 0),
-    ("uT", 4, 2),
-    ("uN", 5, 1),
-    ("uD", 4, 3),
-    ("wQ", 6),
-    ("thG", 3, 128, 256),
     ("uN", 4, 1),
-    ("uR", 4, 3),
     ("uD", 4, 1),
-    ("uN", 5, 2),
-    ("uR", 5, 1),
-    ("thG", 0, 224, 256),
-    ("uN", 5, 3),
-    ("nM", 5),
-    ("uN", 5, 0),
-    ("uT", 5, 1),
-    ("uT", 4, 3),
     ("uR", 4, 1),
-    ("wS", 7, 0),
+    ("uT", 4, 0),
     ("uT", 4, 1),
-    ("uD", 5, 2),
-    ("nM", 6),
-    ("uR", 5, 0),
-    ("uD", 5, 3),
+    ("nM", 4),
+    ("wS", 5, 1),
+    ("nE", 4),
+    ("uN", 4, 2),
+    ("uD", 4, 2),
+    ("wQ", 5),
+    ("uR", 4, 2),
+    ("uT", 4, 2),
+    ("uN", 4, 3),
+    ("uD", 4, 3),
+    ("uR", 4, 3),
+    ("uT", 4, 3),
+    ("thV", 4, 0, 96),
+    ("thG", 4, 96, 256),
+    ("wT", 6),
+    ("uN", 5, 0),
     ("uD", 5, 0),
-    ("uN", 6, 3),
-    ("thV", 1, 0, 160),
-    ("uN", 6, 0),
-    ("uR", 5, 2),
-    ("thG", 2, 64, 256),
-    ("thV", 4, 0, 256),
-    ("uN", 6, 1),
-    ("uD", 6, 0),
-    ("wS", 7, 1),
-    ("wQ", 7),
-    ("nE", 6),
-    ("nM", 7),
-    ("uD", 6, 3),
-    ("thV", 3, 0, 128),
-    ("nE", 5),
-    ("uR", 5, 3),
-    ("uR", 6, 0),
-    ("uR", 6, 3),
-    ("uD", 6, 1),
-    ("nE", 7),
-    ("uR", 6, 1),
-    ("uT", 5, 2),
-    ("uN", 7, 3),
+    ("wS", 6, 0),
+    ("uR", 5, 0),
+    ("uN", 5, 1),
+    ("uD", 5, 1),
+    ("uR", 5, 1),
     ("uT", 5, 0),
-    ("thG", 1, 160, 256),
-    ("uN", 6, 2),
-    ("uN", 7, 0),
+    ("uT", 5, 1),
+    ("nM", 5),
+    ("wS", 6, 1),
+    ("nE", 5),
+    ("uN", 5, 2),
+    ("uD", 5, 2),
+    ("wQ", 6),
+    ("uR", 5, 2),
+    ("uT", 5, 2),
+    ("uN", 5, 3),
+    ("uD", 5, 3),
+    ("uR", 5, 3),
     ("uT", 5, 3),
-    ("uR", 6, 2),
-    ("uD", 6, 2),
-    ("uD", 7, 3),
-    ("thV", 2, 0, 64),
+    ("thV", 5, 0, 96),
+    ("thG", 5, 96, 256),
+    ("wT", 7),
+    ("uN", 6, 0),
+    ("uD", 6, 0),
+    ("wS", 7, 0),
+    ("uR", 6, 0),
+    ("uN", 6, 1),
+    ("uD", 6, 1),
+    ("uR", 6, 1),
     ("uT", 6, 0),
     ("uT", 6, 1),
-    ("uT", 6, 3),
-    ("uN", 7, 2),
-    ("uN", 7, 1),
-    ("uR", 7, 3),
-    ("uD", 7, 0),
-    ("thG", 5, 0, 256),
+    ("nM", 6),
+    ("wS", 7, 1),
+    ("nE", 6),
+    ("uN", 6, 2),
+    ("uD", 6, 2),
+    ("wQ", 7),
+    ("uR", 6, 2),
     ("uT", 6, 2),
-    ("thV", 6, 0, 128),
+    ("uN", 6, 3),
+    ("uD", 6, 3),
+    ("uR", 6, 3),
+    ("uT", 6, 3),
+    ("thV", 6, 0, 32),
+    ("thG", 6, 32, 256),
+    ("uN", 7, 0),
+    ("uD", 7, 0),
     ("uR", 7, 0),
-    ("uT", 7, 3),
-    ("uR", 7, 1),
+    ("uN", 7, 1),
     ("uD", 7, 1),
-    ("uR", 7, 2),
+    ("uR", 7, 1),
     ("uT", 7, 0),
-    ("uD", 7, 2),
     ("uT", 7, 1),
+    ("nM", 7),
+    ("nE", 7),
+    ("uN", 7, 2),
+    ("uD", 7, 2),
+    ("uR", 7, 2),
     ("uT", 7, 2),
-    ("thG", 6, 128, 256),
-    ("thV", 7, 0, 192),
-    ("thG", 7, 192, 256),
+    ("uN", 7, 3),
+    ("uD", 7, 3),
+    ("uR", 7, 3),
+    ("uT", 7, 3),
+    ("thV", 7, 0, 128),
+    ("thV", 7, 128, 256),
 ]
 
 FLOPS = 2 * (2 * B * S + B) * K * D
@@ -251,7 +253,7 @@ def tile_mpl_kernel(tc, p, q, W, out):
         keep = ctx.enter_context(tc.tile_pool(name="keep", bufs=1))
         grp = ctx.enter_context(tc.tile_pool(name="grp", bufs=2))
         epi = ctx.enter_context(tc.tile_pool(name="epi", bufs=3))
-        tpool = ctx.enter_context(tc.tile_pool(name="tpool", bufs=5))
+        tpool = ctx.enter_context(tc.tile_pool(name="tpool", bufs=4))
         ps_tp = ctx.enter_context(tc.psum_pool(name="ps_tp", bufs=3))
         ps_mx = ctx.enter_context(tc.psum_pool(name="ps_mx", bufs=5))
         ctx.enter_context(tc.manual_schedule())
@@ -461,11 +463,11 @@ def tile_mpl_kernel(tc, p, q, W, out):
             )
 
         def thV(c, lo, hi):
-            ov = epi.tile([P, 256 * S], F32, name="ov")
+            ov = epi.tile([P, 192 * S], F32, name="ov")
             third(nc.vector, ov, c, lo, hi)
 
         def thG(c, lo, hi):
-            og = epi.tile([P, 256 * S], F32, name="og")
+            og = epi.tile([P, 224 * S], F32, name="og")
             third(nc.gpsimd, og, c, lo, hi)
 
         steps = {

@@ -95,8 +95,7 @@ SEQ = [
     ("uD", 0, 3),
     ("uR", 0, 3),
     ("uT", 0, 3),
-    ("thV", 0, 0, 192),
-    ("thG", 0, 192, 256),
+    ("thV", 0, 0, 256),
     ("uN", 1, 3),
     ("uD", 1, 3),
     ("uR", 1, 3),
@@ -110,8 +109,7 @@ SEQ = [
     ("uT", 2, 0),
     ("uT", 2, 1),
     ("wQ", 3),
-    ("thV", 1, 0, 192),
-    ("thG", 1, 192, 256),
+    ("thV", 1, 0, 256),
     ("nM", 2),
     ("nE", 2),
     ("uN", 2, 2),
@@ -122,8 +120,7 @@ SEQ = [
     ("uD", 2, 3),
     ("uR", 2, 3),
     ("uT", 2, 3),
-    ("thV", 2, 0, 96),
-    ("thG", 2, 96, 256),
+    ("thV", 2, 0, 256),
     ("wT", 4),
     ("uN", 3, 0),
     ("uD", 3, 0),
@@ -146,8 +143,7 @@ SEQ = [
     ("uD", 3, 3),
     ("uR", 3, 3),
     ("uT", 3, 3),
-    ("thV", 3, 0, 96),
-    ("thG", 3, 96, 256),
+    ("thV", 3, 0, 256),
     ("wT", 5),
     ("uN", 4, 0),
     ("uD", 4, 0),
@@ -170,8 +166,7 @@ SEQ = [
     ("uD", 4, 3),
     ("uR", 4, 3),
     ("uT", 4, 3),
-    ("thV", 4, 0, 96),
-    ("thG", 4, 96, 256),
+    ("thV", 4, 0, 256),
     ("wT", 6),
     ("uN", 5, 0),
     ("uD", 5, 0),
@@ -194,8 +189,7 @@ SEQ = [
     ("uD", 5, 3),
     ("uR", 5, 3),
     ("uT", 5, 3),
-    ("thV", 5, 0, 96),
-    ("thG", 5, 96, 256),
+    ("thV", 5, 0, 256),
     ("wT", 7),
     ("uN", 6, 0),
     ("uD", 6, 0),
@@ -218,8 +212,7 @@ SEQ = [
     ("uD", 6, 3),
     ("uR", 6, 3),
     ("uT", 6, 3),
-    ("thV", 6, 0, 32),
-    ("thG", 6, 32, 256),
+    ("thV", 6, 0, 256),
     ("uN", 7, 0),
     ("uD", 7, 0),
     ("uR", 7, 0),
@@ -463,11 +456,11 @@ def tile_mpl_kernel(tc, p, q, W, out):
             )
 
         def thV(c, lo, hi):
-            ov = epi.tile([P, 192 * S], F32, name="ov")
+            ov = epi.tile([P, 256 * S], F32, name="ov")
             third(nc.vector, ov, c, lo, hi)
 
         def thG(c, lo, hi):
-            og = epi.tile([P, 224 * S], F32, name="og")
+            og = epi.tile([P, 32 * S], F32, name="og")
             third(nc.gpsimd, og, c, lo, hi)
 
         steps = {

@@ -13,461 +13,256 @@ ALU = mybir.AluOpType
 
 P = 128
 B, S, D, K = 128, 8, 1024, 2048
-KC = 256
-NCH = K // KC
-NSP = S // 2
-PC = ["S","S","S","S"]
-WM = ["SV","S","S","S","S","S","S","S"]
-LOADS = ["w0","p0","q","w1","p1","w2","w3","p2","p3","w4","w5","w6","w7"]
-SEQ = [
-    ("wT", 0),
-    ("pT", 0),
-    ("qT",),
-    ("wS", 0, 0),
-    ("wS", 0, 1),
-    ("pC", 0),
-    ("qC",),
-    ("qS",),
-    ("pT", 1),
-    ("wQ", 0),
-    ("pP", 0),
-    ("pR", 0),
-    ("pQ", 0),
-    ("qQ",),
-    ("pC", 1),
-    ("wT", 1),
-    ("wS", 1, 0),
-    ("wS", 1, 1),
-    ("pP", 1),
-    ("pR", 1),
-    ("pU", 0),
-    ("pU", 1),
-    ("wQ", 1),
-    ("pT", 2),
-    ("pC", 2),
-    ("wT", 2),
-    ("wS", 2, 0),
-    ("pT", 3),
-    ("pC", 3),
-    ("pP", 2),
-    ("pR", 2),
-    ("pQ", 2),
-    ("pQ", 1),
-    ("pP", 3),
-    ("pR", 3),
-    ("nM", 0),
-    ("nM", 1),
-    ("nE", 0),
-    ("nE", 1),
-    ("uN", 0, 0),
-    ("uD", 0, 0),
-    ("uR", 0, 0),
-    ("wS", 2, 1),
-    ("uN", 1, 0),
-    ("uD", 1, 0),
-    ("uR", 1, 0),
-    ("uT", 0, 0),
-    ("pU", 2),
-    ("uT", 1, 0),
-    ("pU", 3),
-    ("uN", 0, 1),
-    ("uD", 0, 1),
-    ("wT", 3),
-    ("wS", 3, 0),
-    ("uR", 0, 1),
-    ("uN", 1, 1),
-    ("uD", 1, 1),
-    ("uR", 1, 1),
-    ("uT", 0, 1),
-    ("uT", 1, 1),
-    ("pQ", 3),
-    ("wQ", 2),
-    ("uN", 0, 2),
-    ("uD", 0, 2),
-    ("uR", 0, 2),
-    ("wS", 3, 1),
-    ("uN", 1, 2),
-    ("uD", 1, 2),
-    ("uR", 1, 2),
-    ("uT", 0, 2),
-    ("uT", 1, 2),
-    ("uN", 0, 3),
-    ("uD", 0, 3),
-    ("uR", 0, 3),
-    ("uT", 0, 3),
-    ("thV", 0, 0, 256),
-    ("uN", 1, 3),
-    ("uD", 1, 3),
-    ("uR", 1, 3),
-    ("uT", 1, 3),
-    ("uN", 2, 0),
-    ("uD", 2, 0),
-    ("uR", 2, 0),
-    ("uN", 2, 1),
-    ("uD", 2, 1),
-    ("uR", 2, 1),
-    ("uT", 2, 0),
-    ("uT", 2, 1),
-    ("wQ", 3),
-    ("thV", 1, 0, 256),
-    ("nM", 2),
-    ("nE", 2),
-    ("uN", 2, 2),
-    ("uD", 2, 2),
-    ("uR", 2, 2),
-    ("uT", 2, 2),
-    ("uN", 2, 3),
-    ("uD", 2, 3),
-    ("uR", 2, 3),
-    ("uT", 2, 3),
-    ("thV", 2, 0, 256),
-    ("wT", 4),
-    ("uN", 3, 0),
-    ("uD", 3, 0),
-    ("wS", 4, 0),
-    ("uR", 3, 0),
-    ("uN", 3, 1),
-    ("uD", 3, 1),
-    ("uR", 3, 1),
-    ("uT", 3, 0),
-    ("uT", 3, 1),
-    ("nM", 3),
-    ("wS", 4, 1),
-    ("nE", 3),
-    ("uN", 3, 2),
-    ("uD", 3, 2),
-    ("wQ", 4),
-    ("uR", 3, 2),
-    ("uT", 3, 2),
-    ("uN", 3, 3),
-    ("uD", 3, 3),
-    ("uR", 3, 3),
-    ("uT", 3, 3),
-    ("thV", 3, 0, 256),
-    ("wT", 5),
-    ("uN", 4, 0),
-    ("uD", 4, 0),
-    ("wS", 5, 0),
-    ("uR", 4, 0),
-    ("uN", 4, 1),
-    ("uD", 4, 1),
-    ("uR", 4, 1),
-    ("uT", 4, 0),
-    ("uT", 4, 1),
-    ("nM", 4),
-    ("wS", 5, 1),
-    ("nE", 4),
-    ("uN", 4, 2),
-    ("uD", 4, 2),
-    ("wQ", 5),
-    ("uR", 4, 2),
-    ("uT", 4, 2),
-    ("uN", 4, 3),
-    ("uD", 4, 3),
-    ("uR", 4, 3),
-    ("uT", 4, 3),
-    ("thV", 4, 0, 256),
-    ("wT", 6),
-    ("uN", 5, 0),
-    ("uD", 5, 0),
-    ("wS", 6, 0),
-    ("uR", 5, 0),
-    ("uN", 5, 1),
-    ("uD", 5, 1),
-    ("uR", 5, 1),
-    ("uT", 5, 0),
-    ("uT", 5, 1),
-    ("nM", 5),
-    ("wS", 6, 1),
-    ("nE", 5),
-    ("uN", 5, 2),
-    ("uD", 5, 2),
-    ("wQ", 6),
-    ("uR", 5, 2),
-    ("uT", 5, 2),
-    ("uN", 5, 3),
-    ("uD", 5, 3),
-    ("uR", 5, 3),
-    ("uT", 5, 3),
-    ("thV", 5, 0, 256),
-    ("wT", 7),
-    ("uN", 6, 0),
-    ("uD", 6, 0),
-    ("wS", 7, 0),
-    ("uR", 6, 0),
-    ("uN", 6, 1),
-    ("uD", 6, 1),
-    ("uR", 6, 1),
-    ("uT", 6, 0),
-    ("uT", 6, 1),
-    ("nM", 6),
-    ("wS", 7, 1),
-    ("nE", 6),
-    ("uN", 6, 2),
-    ("uD", 6, 2),
-    ("wQ", 7),
-    ("uR", 6, 2),
-    ("uT", 6, 2),
-    ("uN", 6, 3),
-    ("uD", 6, 3),
-    ("uR", 6, 3),
-    ("uT", 6, 3),
-    ("thV", 6, 0, 256),
-    ("uN", 7, 0),
-    ("uD", 7, 0),
-    ("uR", 7, 0),
-    ("uN", 7, 1),
-    ("uD", 7, 1),
-    ("uR", 7, 1),
-    ("uT", 7, 0),
-    ("uT", 7, 1),
-    ("nM", 7),
-    ("nE", 7),
-    ("uN", 7, 2),
-    ("uD", 7, 2),
-    ("uR", 7, 2),
-    ("uT", 7, 2),
-    ("uN", 7, 3),
-    ("uD", 7, 3),
-    ("uR", 7, 3),
-    ("uT", 7, 3),
-    ("thV", 7, 0, 128),
-    ("thV", 7, 128, 256),
-]
+PASSES = D // (4 * P)
+K_CHUNK = 256
+CHUNKS = K // K_CHUNK
+PAIRS = S // 2
+UNITS = CHUNKS * PAIRS
+AHEAD = 2
 
 FLOPS = 2 * (2 * B * S + B) * K * D
 
 
 def tile_mpl_kernel(tc, p, q, W, out):
     nc = tc.nc
-    out_flat = out.rearrange("b s k -> b (s k)")
+    out_rows = out.rearrange("b s k -> b (s k)")
     with ExitStack() as ctx:
-        const = ctx.enter_context(tc.tile_pool(name="const", bufs=1))
-        keep = ctx.enter_context(tc.tile_pool(name="keep", bufs=1))
-        grp = ctx.enter_context(tc.tile_pool(name="grp", bufs=2))
-        epi = ctx.enter_context(tc.tile_pool(name="epi", bufs=3))
-        tpool = ctx.enter_context(tc.tile_pool(name="tpool", bufs=4))
-        ps_tp = ctx.enter_context(tc.psum_pool(name="ps_tp", bufs=3))
-        ps_mx = ctx.enter_context(tc.psum_pool(name="ps_mx", bufs=5))
+        inputs = ctx.enter_context(tc.tile_pool(name="inputs", bufs=1))
+        operands = ctx.enter_context(tc.tile_pool(name="operands", bufs=1))
+        staging = ctx.enter_context(tc.tile_pool(name="staging", bufs=2))
+        results = ctx.enter_context(tc.tile_pool(name="results", bufs=3))
+        flip_banks = ctx.enter_context(tc.psum_pool(name="flip_banks", bufs=2))
+        sum_banks = ctx.enter_context(tc.psum_pool(name="sum_banks", bufs=6))
         ctx.enter_context(tc.manual_schedule())
 
-        q_sb = const.tile([P, D], BF16, name="q_sb")
-        p_sb = [const.tile([P, 2, D], BF16, name="p_sb%d" % sp) for sp in range(NSP)]
-        w_sb = [const.tile([P, 2, D], BF16, name="w_sb%d" % c) for c in range(NCH)]
-        for name in LOADS:
-            i = int(name[1:]) if len(name) > 1 else 0
-            if name[0] == "q":
-                nc.sync.dma_start(out=q_sb[:], in_=q[:, S - 1, :])
-            elif name[0] == "p":
-                nc.sync.dma_start(out=p_sb[i][:], in_=p[:, 2 * i : 2 * i + 2, :])
-            else:
-                nc.sync.dma_start(
-                    out=w_sb[i][:], in_=W[KC * i : KC * (i + 1), :].rearrange("(t r) d -> r t d", r=P)
-                )
+        q_rows = inputs.tile([P, D], BF16, name="q_rows")
+        p_rows = [inputs.tile([P, 2, D], BF16, name="p_rows%d" % pair) for pair in range(PAIRS)]
+        w_rows = [inputs.tile([P, 2, D], BF16, name="w_rows%d" % c) for c in range(CHUNKS)]
 
-        ident = const.tile([P, P], F32, name="ident")
-        make_identity(nc, ident[:])
-        one = const.tile([P, 1], F32, name="one")
+        def load_p(pair):
+            nc.sync.dma_start(out=p_rows[pair][:], in_=p[:, 2 * pair : 2 * pair + 2, :])
+
+        def load_w(c):
+            rows = W[K_CHUNK * c : K_CHUNK * (c + 1), :]
+            nc.sync.dma_start(out=w_rows[c][:], in_=rows.rearrange("(t r) d -> r t d", r=P))
+
+        load_w(0)
+        load_p(0)
+        nc.sync.dma_start(out=q_rows[:], in_=q[:, S - 1, :])
+        for pair in range(1, PAIRS):
+            load_p(pair)
+        for c in range(1, CHUNKS):
+            load_w(c)
+
+        identity = inputs.tile([P, P], F32, name="identity")
+        make_identity(nc, identity[:])
+        one = inputs.tile([P, 1], F32, name="one")
         nc.vector.memset(one[:], 1.0)
-        warm = const.tile([P, 1], F32, name="warm")
+        warm = inputs.tile([P, 1], F32, name="warm")
         nc.scalar.activation(out=warm[:], in_=one[:], func=ACT.Abs_reciprocal_sqrt)
 
-        qg = const.tile([P, 2, 512], BF16, name="qg")
-        gq = const.tile([P, 1024], BF16, name="gq", align_bytes=64)
-        qc = keep.tile([P, 256], U32, name="qc", align_bytes=64)
-        qs = keep.tile([P, 256], U8, name="qs", align_bytes=64)
-        pqc = [keep.tile([P, 512], U32, name="pqc%d" % sp, align_bytes=64) for sp in range(NSP)]
-        pqs = [keep.tile([P, 512], U8, name="pqs%d" % sp, align_bytes=64) for sp in range(NSP)]
-        ppc = [keep.tile([P, 512], U32, name="ppc%d" % sp, align_bytes=64) for sp in range(NSP)]
-        pps = [keep.tile([P, 512], U8, name="pps%d" % sp, align_bytes=64) for sp in range(NSP)]
-        wc = [keep.tile([P, 512], U32, name="wc%d" % c, align_bytes=64) for c in range(NCH)]
-        ws = [keep.tile([P, 512], U8, name="ws%d" % c, align_bytes=64) for c in range(NCH)]
-        T = {}
+        q_flipped = inputs.tile([P, PASSES, 4 * P], BF16, name="q_flipped")
+        qq_values = inputs.tile([P, PASSES * 4 * P], BF16, name="qq_values", align_bytes=64)
+        qq_codes = operands.tile([P, PASSES * P], U32, name="qq_codes", align_bytes=64)
+        qq_scales = operands.tile([P, PASSES * P], U8, name="qq_scales", align_bytes=64)
+        pq_codes = [operands.tile([P, 512], U32, name="pq_codes%d" % i, align_bytes=64) for i in range(PAIRS)]
+        pq_scales = [operands.tile([P, 512], U8, name="pq_scales%d" % i, align_bytes=64) for i in range(PAIRS)]
+        pp_codes = [operands.tile([P, 512], U32, name="pp_codes%d" % i, align_bytes=64) for i in range(PAIRS)]
+        pp_scales = [operands.tile([P, 512], U8, name="pp_scales%d" % i, align_bytes=64) for i in range(PAIRS)]
+        w2_codes = [operands.tile([P, 512], U32, name="w2_codes%d" % c, align_bytes=64) for c in range(CHUNKS)]
+        w2_scales = [operands.tile([P, 512], U8, name="w2_scales%d" % c, align_bytes=64) for c in range(CHUNKS)]
+        q_factor = [operands.tile([P, K_CHUNK], F32, name="q_factor%d" % c) for c in range(CHUNKS)]
+        live = {}
 
-        def transposes(bank, rows, g):
+        def flip(rows, g):
+            bank = flip_banks.tile([P, 512], F32, name="flipped")
             for u in range(2):
                 for t in range(2):
                     nc.tensor.transpose(
                         out=bank[:, u * 256 + t * P : u * 256 + (t + 1) * P],
                         in_=rows[:, t, :].bitcast(F32)[:, 256 * g + P * u : 256 * g + P * (u + 1)],
-                        identity=ident[:],
+                        identity=identity[:],
                     )
+            return bank
 
-        def words_out(eng, dst, bank):
-            src = bank[:].rearrange("p (u n) -> p n u", u=2)
-            dstw = dst.bitcast(F32).rearrange("p (n u) -> p n u", u=2)
-            if eng == "S":
-                nc.scalar.copy(out=dstw, in_=src)
-            else:
-                nc.vector.tensor_copy(out=dstw, in_=src)
+        def copy_words(dst, bank):
+            nc.scalar.copy(
+                out=dst.bitcast(F32).rearrange("p (n u) -> p n u", u=2),
+                in_=bank[:].rearrange("p (u n) -> p n u", u=2),
+            )
 
-        def square_out(dst, bank):
+        def square_words(dst, bank):
             nc.scalar.activation(
                 out=dst.rearrange("p (n u e) -> p n u e", u=2, e=2),
                 in_=bank[:].bitcast(BF16).rearrange("p (u n e) -> p n u e", u=2, e=2),
                 func=ACT.Square,
             )
 
-        def quant(codes, scales, src):
-            nc.vector.quantize_mx(out=codes[:].bitcast(FP8X4), scales=scales[:], in_=src)
+        def quantise(codes, scales, values):
+            nc.vector.quantize_mx(out=codes[:].bitcast(FP8X4), scales=scales[:], in_=values)
 
-        def qT():
-            bank = ps_tp.tile([P, 512], F32, name="tb", tag="tb")
-            T["qb"] = bank
+        def q_flip():
+            bank = flip_banks.tile([P, 512], F32, name="flipped")
             for u in range(2):
-                for g in range(2):
+                for g in range(PASSES):
                     nc.tensor.transpose(
                         out=bank[:, u * 256 + g * P : u * 256 + (g + 1) * P],
-                        in_=q_sb[:].bitcast(F32)[:, 256 * g + P * u : 256 * g + P * (u + 1)],
-                        identity=ident[:],
+                        in_=q_rows[:].bitcast(F32)[:, 256 * g + P * u : 256 * g + P * (u + 1)],
+                        identity=identity[:],
                     )
+            live["q"] = bank
 
-        def qC():
-            words_out("S", qg[:].rearrange("p g n -> p (g n)"), T["qb"])
+        def p_flip(pair):
+            for g in range(PASSES):
+                live["p", pair, g] = flip(p_rows[pair], g)
 
-        def qS():
-            square_out(gq[:], T["qb"])
+        def p_copy(pair):
+            flipped = staging.tile([P, PASSES, 1024], BF16, name="p_flipped")
+            live["p_flipped", pair] = flipped
+            for g in range(PASSES):
+                copy_words(flipped[:, g, :], live["p", pair, g])
 
-        def qQ():
-            quant(qc, qs, gq[:])
+        def p_square(pair):
+            values = staging.tile([P, PASSES * 1024], BF16, name="pp_values", align_bytes=64)
+            flat = live["p_flipped", pair][:].rearrange("p g n -> p (g n)")
+            nc.vector.tensor_tensor(out=values[:], in0=flat, in1=flat, op=ALU.mult)
+            quantise(pp_codes[pair], pp_scales[pair], values[:])
 
-        def pT(sp):
-            for g in range(2):
-                bank = ps_tp.tile([P, 512], F32, name="tb", tag="tb")
-                T["pb", sp, g] = bank
-                transposes(bank, p_sb[sp], g)
-
-        def pC(sp):
-            pt = grp.tile([P, 2, 1024], BF16, name="pt")
-            T["pt", sp] = pt
-            for g in range(2):
-                words_out(PC[sp], pt[:, g, :], T["pb", sp, g])
-
-        def pP(sp):
-            gpp = grp.tile([P, 2048], BF16, name="gpp", align_bytes=64)
-            T["gpp", sp] = gpp
-            flat = T["pt", sp][:].rearrange("p g n -> p (g n)")
-            nc.vector.tensor_tensor(out=gpp[:], in0=flat, in1=flat, op=ALU.mult)
-
-        def pR(sp):
-            gpq = grp.tile([P, 2, 1024], BF16, name="gpq", align_bytes=64)
-            T["gpq", sp] = gpq
-            for g in range(2):
+        def p_times_q(pair):
+            values = staging.tile([P, PASSES, 1024], BF16, name="pq_values", align_bytes=64)
+            for g in range(PASSES):
                 nc.vector.tensor_tensor(
-                    out=gpq[:, g, :].rearrange("p (s n) -> p s n", s=2),
-                    in0=T["pt", sp][:, g, :].rearrange("p (s n) -> p s n", s=2),
-                    in1=qg[:, g, :].unsqueeze(1).to_broadcast([P, 2, 512]),
+                    out=values[:, g, :].rearrange("p (s n) -> p s n", s=2),
+                    in0=live["p_flipped", pair][:, g, :].rearrange("p (s n) -> p s n", s=2),
+                    in1=q_flipped[:, g, :].unsqueeze(1).to_broadcast([P, 2, 4 * P]),
                     op=ALU.mult,
                 )
+            quantise(pq_codes[pair], pq_scales[pair], values[:].rearrange("p g n -> p (g n)"))
 
-        def pQ(sp):
-            quant(ppc[sp], pps[sp], T["gpp", sp][:])
+        def w_flip(c):
+            for g in range(PASSES):
+                live["w", c, g] = flip(w_rows[c], g)
 
-        def pU(sp):
-            quant(pqc[sp], pqs[sp], T["gpq", sp][:].rearrange("p g n -> p (g n)"))
-
-        def wT(c):
-            for g in range(2):
-                bank = ps_tp.tile([P, 512], F32, name="tb", tag="tb")
-                T["wb", c, g] = bank
-                transposes(bank, w_sb[c], g)
-
-        def wS(c, g):
+        def w_square(c, g):
             if g == 0:
-                T["gw", c] = grp.tile([P, 2, 1024], BF16, name="gw", align_bytes=64)
-            gw = T["gw", c]
-            if WM[c] == "S":
-                square_out(gw[:, g, :], T["wb", c, g])
+                live["w2", c] = staging.tile([P, PASSES, 1024], BF16, name="w2_values", align_bytes=64)
+            values = live["w2", c]
+            if c == 0:
+                flipped = staging.tile([P, 1024], BF16, name="w_flipped")
+                copy_words(flipped[:], live["w", c, g])
+                nc.vector.tensor_tensor(out=values[:, g, :], in0=flipped[:], in1=flipped[:], op=ALU.mult)
             else:
-                wt = grp.tile([P, 1024], BF16, name="wt")
-                words_out(WM[c][0], wt[:], T["wb", c, g])
-                nc.vector.tensor_tensor(out=gw[:, g, :], in0=wt[:], in1=wt[:], op=ALU.mult)
+                square_words(values[:, g, :], live["w", c, g])
 
-        def wQ(c):
-            quant(wc[c], ws[c], T["gw", c][:].rearrange("p g n -> p (g n)"))
+        def w_quantise(c):
+            quantise(w2_codes[c], w2_scales[c], live["w2", c][:].rearrange("p g n -> p (g n)"))
 
-        def group(dst, lc, ls, first, c):
-            for g in range(2):
-                col = (first + 2 * g) * P if first >= 0 else g * P
+        def contract(sums, codes, scales, first, step, c):
+            for g in range(PASSES):
+                cols = slice((first + step * g) * P, (first + step * g + 1) * P)
+                k_cols = slice(g * K_CHUNK, (g + 1) * K_CHUNK)
                 nc.tensor.matmul_mx(
-                    out=dst,
-                    lhsT=lc[:, col : col + P].bitcast(FP8X4),
-                    lhsT_scale=ls[:, col : col + P],
-                    rhs=wc[c][:, g * KC : (g + 1) * KC].bitcast(FP8X4),
-                    rhs_scale=ws[c][:, g * KC : (g + 1) * KC],
+                    out=sums,
+                    lhsT=codes[:, cols].bitcast(FP8X4),
+                    lhsT_scale=scales[:, cols],
+                    rhs=w2_codes[c][:, k_cols].bitcast(FP8X4),
+                    rhs_scale=w2_scales[c][:, k_cols],
                     start=(g == 0),
-                    stop=(g == 1),
+                    stop=(g == PASSES - 1),
                 )
 
-        def nM(c):
-            bank = ps_mx.tile([P, 512], F32, name="mb", tag="mb")
-            T["nq", c] = bank
-            group(bank[:, 0:KC], qc, qs, -1, c)
-
-        def nE(c):
-            rq = keep.tile([P, KC], F32, name="rq%d" % c)
-            T["rq", c] = rq
+        def q_norm(c):
+            bank = sum_banks.tile([P, 512], F32, name="sums")
+            contract(bank[:, 0:K_CHUNK], qq_codes, qq_scales, 0, 1, c)
             nc.scalar.activation(
-                out=rq[:], in_=T["nq", c][:, 0:KC], func=ACT.Abs_reciprocal_sqrt, scale=float(D * D)
+                out=q_factor[c][:], in_=bank[:, 0:K_CHUNK], func=ACT.Abs_reciprocal_sqrt, scale=float(D * D)
             )
 
-        def uN(c, sp):
-            bank = ps_mx.tile([P, 512], F32, name="mb", tag="mb")
-            T["nb", c, sp] = bank
+        def p_norms(unit):
+            c, pair = divmod(unit, PAIRS)
+            bank = sum_banks.tile([P, 512], F32, name="sums")
             for s in range(2):
-                group(bank[:, s * KC : (s + 1) * KC], ppc[sp], pps[sp], s, c)
-
-        def uD(c, sp):
-            bank = ps_mx.tile([P, 512], F32, name="mb", tag="mb")
-            T["db", c, sp] = bank
-            for s in range(2):
-                group(bank[:, s * KC : (s + 1) * KC], pqc[sp], pqs[sp], s, c)
-
-        def uR(c, sp):
-            r = epi.tile([P, 2 * KC], F32, name="r")
-            T["r", c, sp] = r
+                contract(bank[:, s * K_CHUNK : (s + 1) * K_CHUNK], pp_codes[pair], pp_scales[pair], s, 2, c)
+            factor = results.tile([P, 2 * K_CHUNK], F32, name="p_factor")
+            live["p_factor", unit] = factor
             nc.scalar.activation(
-                out=r[:].rearrange("p (k s) -> p k s", s=2),
-                in_=T["nb", c, sp][:].rearrange("p (s k) -> p k s", s=2),
+                out=factor[:].rearrange("p (k s) -> p k s", s=2),
+                in_=bank[:].rearrange("p (s k) -> p k s", s=2),
                 func=ACT.Abs_reciprocal_sqrt,
             )
 
-        def uT(c, sp):
-            if ("tt", c) not in T:
-                T["tt", c] = tpool.tile([P, NSP, 2 * KC], F32, name="tt")
+        def dots(unit):
+            c, pair = divmod(unit, PAIRS)
+            bank = sum_banks.tile([P, 512], F32, name="sums")
+            for s in range(2):
+                contract(bank[:, s * K_CHUNK : (s + 1) * K_CHUNK], pq_codes[pair], pq_scales[pair], s, 2, c)
+            if pair == 0:
+                live["cosines", c] = results.tile([P, PAIRS, 2 * K_CHUNK], F32, name="cosines")
             nc.vector.scalar_tensor_tensor(
-                out=T["tt", c][:, sp, :].rearrange("p (k s) -> p k s", s=2),
-                in0=T["db", c, sp][:].rearrange("p (s k) -> p k s", s=2),
+                out=live["cosines", c][:, pair, :].rearrange("p (k s) -> p k s", s=2),
+                in0=bank[:].rearrange("p (s k) -> p k s", s=2),
                 scalar=-1.0,
-                in1=T["r", c, sp][:].rearrange("p (k s) -> p k s", s=2),
+                in1=live["p_factor", unit][:].rearrange("p (k s) -> p k s", s=2),
                 op0=ALU.mult,
                 op1=ALU.mult,
             )
 
-        def third(eng, o, c, lo, hi):
-            eng.tensor_tensor(
-                out=o[:, 0 : (hi - lo) * S].rearrange("p (k a s) -> p k a s", a=NSP, s=2),
-                in0=T["tt", c][:].rearrange("p a (k s) -> p k a s", s=2)[:, lo:hi, :, :],
-                in1=T["rq", c][:, lo:hi].unsqueeze(2).unsqueeze(3).to_broadcast([P, hi - lo, NSP, 2]),
+        def finish(c, lo, hi):
+            dist = results.tile([P, K_CHUNK * S], F32, name="dist")
+            nc.vector.tensor_tensor(
+                out=dist[:, 0 : (hi - lo) * S].rearrange("p (k a s) -> p k a s", a=PAIRS, s=2),
+                in0=live["cosines", c][:].rearrange("p a (k s) -> p k a s", s=2)[:, lo:hi, :, :],
+                in1=q_factor[c][:, lo:hi].unsqueeze(2).unsqueeze(3).to_broadcast([P, hi - lo, PAIRS, 2]),
                 op=ALU.mult,
             )
             nc.sync.dma_start(
-                out=out_flat[:, (c * KC + lo) * S : (c * KC + hi) * S], in_=o[:, 0 : (hi - lo) * S]
+                out=out_rows[:, (c * K_CHUNK + lo) * S : (c * K_CHUNK + hi) * S], in_=dist[:, 0 : (hi - lo) * S]
             )
 
-        def thV(c, lo, hi):
-            ov = epi.tile([P, 256 * S], F32, name="ov")
-            third(nc.vector, ov, c, lo, hi)
+        w_flip(0)
+        p_flip(0)
+        q_flip()
+        w_square(0, 0)
+        w_square(0, 1)
+        p_copy(0)
+        square_words(qq_values[:], live["q"])
+        copy_words(q_flipped[:].rearrange("p g n -> p (g n)"), live["q"])
+        w_quantise(0)
+        for pair in range(PAIRS):
+            if pair > 0:
+                p_copy(pair)
+            if pair + 1 < PAIRS:
+                p_flip(pair + 1)
+            p_square(pair)
+            if pair == 0:
+                quantise(qq_codes, qq_scales, qq_values[:])
+            p_times_q(pair)
+        q_norm(0)
+        w_flip(1)
+        w_square(1, 0)
+        w_square(1, 1)
+        w_quantise(1)
 
-        def thG(c, lo, hi):
-            og = epi.tile([P, 32 * S], F32, name="og")
-            third(nc.gpsimd, og, c, lo, hi)
-
-        steps = {
-            "qT": qT, "qC": qC, "qS": qS, "qQ": qQ,
-            "pT": pT, "pC": pC, "pP": pP, "pR": pR, "pQ": pQ, "pU": pU,
-            "wT": wT, "wS": wS, "wQ": wQ, "nM": nM, "nE": nE,
-            "uN": uN, "uD": uD, "uR": uR, "uT": uT, "thV": thV, "thG": thG,
-        }
-        for step in SEQ:
-            steps[step[0]](*step[1:])
+        p_norms(0)
+        for unit in range(UNITS):
+            c, pair = divmod(unit, PAIRS)
+            prepare = c + AHEAD < CHUNKS
+            if pair == 0:
+                if prepare:
+                    w_flip(c + AHEAD)
+                    w_square(c + AHEAD, 0)
+                if c > 0:
+                    q_norm(c)
+            if pair == 1 and prepare:
+                w_square(c + AHEAD, 1)
+            if unit + 1 < UNITS:
+                p_norms(unit + 1)
+            dots(unit)
+            if pair == 1 and prepare:
+                w_quantise(c + AHEAD)
+            if pair == PAIRS - 1:
+                if c + 1 < CHUNKS:
+                    finish(c, 0, K_CHUNK)
+                else:
+                    finish(c, 0, K_CHUNK // 2)
+                    finish(c, K_CHUNK // 2, K_CHUNK)

@@ -19,6 +19,8 @@ CHUNKS = K // K_CHUNK
 PAIRS = S // 2
 UNITS = CHUNKS * PAIRS
 AHEAD = 2
+SQUARE_ON_SCALAR = (False, True, True, False)
+NORMS_AHEAD = False
 
 FLOPS = 2 * (2 * B * S + B) * K * D
 
@@ -31,8 +33,7 @@ def tile_mpl_kernel(tc, p, q, W, out):
         operands = ctx.enter_context(tc.tile_pool(name="operands", bufs=1))
         staging = ctx.enter_context(tc.tile_pool(name="staging", bufs=2))
         results = ctx.enter_context(tc.tile_pool(name="results", bufs=3))
-        flip_banks = ctx.enter_context(tc.psum_pool(name="flip_banks", bufs=2))
-        sum_banks = ctx.enter_context(tc.psum_pool(name="sum_banks", bufs=6))
+        banks = ctx.enter_context(tc.psum_pool(name="banks", bufs=8))
         ctx.enter_context(tc.manual_schedule())
 
         q_rows = inputs.tile([P, D], BF16, name="q_rows")
@@ -75,7 +76,7 @@ def tile_mpl_kernel(tc, p, q, W, out):
         live = {}
 
         def flip(rows, g):
-            bank = flip_banks.tile([P, 512], F32, name="flipped")
+            bank = banks.tile([P, 512], F32, name="bank")
             for u in range(2):
                 for t in range(2):
                     nc.tensor.transpose(
@@ -102,7 +103,7 @@ def tile_mpl_kernel(tc, p, q, W, out):
             nc.vector.quantize_mx(out=codes[:].bitcast(FP8X4), scales=scales[:], in_=values)
 
         def q_flip():
-            bank = flip_banks.tile([P, 512], F32, name="flipped")
+            bank = banks.tile([P, 512], F32, name="bank")
             for u in range(2):
                 for g in range(PASSES):
                     nc.tensor.transpose(
@@ -117,6 +118,8 @@ def tile_mpl_kernel(tc, p, q, W, out):
                 live["p", pair, g] = flip(p_rows[pair], g)
 
         def p_copy(pair):
+            if SQUARE_ON_SCALAR[pair]:
+                return
             flipped = staging.tile([P, PASSES, 1024], BF16, name="p_flipped")
             live["p_flipped", pair] = flipped
             for g in range(PASSES):
@@ -124,19 +127,34 @@ def tile_mpl_kernel(tc, p, q, W, out):
 
         def p_square(pair):
             values = staging.tile([P, PASSES * 1024], BF16, name="pp_values", align_bytes=64)
-            flat = live["p_flipped", pair][:].rearrange("p g n -> p (g n)")
-            nc.vector.tensor_tensor(out=values[:], in0=flat, in1=flat, op=ALU.mult)
+            if SQUARE_ON_SCALAR[pair]:
+                for g in range(PASSES):
+                    square_words(values[:, g * 1024 : (g + 1) * 1024], live["p", pair, g])
+            else:
+                flat = live["p_flipped", pair][:].rearrange("p g n -> p (g n)")
+                nc.vector.tensor_tensor(out=values[:], in0=flat, in1=flat, op=ALU.mult)
             quantise(pp_codes[pair], pp_scales[pair], values[:])
 
         def p_times_q(pair):
             values = staging.tile([P, PASSES, 1024], BF16, name="pq_values", align_bytes=64)
             for g in range(PASSES):
-                nc.vector.tensor_tensor(
-                    out=values[:, g, :].rearrange("p (s n) -> p s n", s=2),
-                    in0=live["p_flipped", pair][:, g, :].rearrange("p (s n) -> p s n", s=2),
-                    in1=q_flipped[:, g, :].unsqueeze(1).to_broadcast([P, 2, 4 * P]),
-                    op=ALU.mult,
-                )
+                if SQUARE_ON_SCALAR[pair]:
+                    nc.vector.tensor_tensor(
+                        out=values[:, g, :].rearrange("p (s n u e) -> p s n u e", s=2, u=2, e=2),
+                        in0=live["p", pair, g][:].bitcast(BF16).rearrange("p (u s n e) -> p s n u e", u=2, s=2, e=2),
+                        in1=q_flipped[:, g, :]
+                        .rearrange("p (n u e) -> p n u e", u=2, e=2)
+                        .unsqueeze(1)
+                        .to_broadcast([P, 2, P, 2, 2]),
+                        op=ALU.mult,
+                    )
+                else:
+                    nc.vector.tensor_tensor(
+                        out=values[:, g, :].rearrange("p (s n) -> p s n", s=2),
+                        in0=live["p_flipped", pair][:, g, :].rearrange("p (s n) -> p s n", s=2),
+                        in1=q_flipped[:, g, :].unsqueeze(1).to_broadcast([P, 2, 4 * P]),
+                        op=ALU.mult,
+                    )
             quantise(pq_codes[pair], pq_scales[pair], values[:].rearrange("p g n -> p (g n)"))
 
         def w_flip(c):
@@ -172,7 +190,7 @@ def tile_mpl_kernel(tc, p, q, W, out):
                 )
 
         def q_norm(c):
-            bank = sum_banks.tile([P, 512], F32, name="sums")
+            bank = banks.tile([P, 512], F32, name="bank")
             contract(bank[:, 0:K_CHUNK], qq_codes, qq_scales, 0, 1, c)
             nc.scalar.activation(
                 out=q_factor[c][:], in_=bank[:, 0:K_CHUNK], func=ACT.Abs_reciprocal_sqrt, scale=float(D * D)
@@ -180,7 +198,7 @@ def tile_mpl_kernel(tc, p, q, W, out):
 
         def p_norms(unit):
             c, pair = divmod(unit, PAIRS)
-            bank = sum_banks.tile([P, 512], F32, name="sums")
+            bank = banks.tile([P, 512], F32, name="bank")
             for s in range(2):
                 contract(bank[:, s * K_CHUNK : (s + 1) * K_CHUNK], pp_codes[pair], pp_scales[pair], s, 2, c)
             factor = results.tile([P, 2 * K_CHUNK], F32, name="p_factor")
@@ -193,7 +211,7 @@ def tile_mpl_kernel(tc, p, q, W, out):
 
         def dots(unit):
             c, pair = divmod(unit, PAIRS)
-            bank = sum_banks.tile([P, 512], F32, name="sums")
+            bank = banks.tile([P, 512], F32, name="bank")
             for s in range(2):
                 contract(bank[:, s * K_CHUNK : (s + 1) * K_CHUNK], pq_codes[pair], pq_scales[pair], s, 2, c)
             if pair == 0:
@@ -243,7 +261,8 @@ def tile_mpl_kernel(tc, p, q, W, out):
         w_square(1, 1)
         w_quantise(1)
 
-        p_norms(0)
+        if NORMS_AHEAD:
+            p_norms(0)
         for unit in range(UNITS):
             c, pair = divmod(unit, PAIRS)
             prepare = c + AHEAD < CHUNKS
@@ -255,7 +274,9 @@ def tile_mpl_kernel(tc, p, q, W, out):
                     q_norm(c)
             if pair == 1 and prepare:
                 w_square(c + AHEAD, 1)
-            if unit + 1 < UNITS:
+            if not NORMS_AHEAD:
+                p_norms(unit)
+            elif unit + 1 < UNITS:
                 p_norms(unit + 1)
             dots(unit)
             if pair == 1 and prepare:

@@ -19,7 +19,7 @@ CHUNKS = K // K_CHUNK
 PAIRS = S // 2
 UNITS = CHUNKS * PAIRS
 AHEAD = 2
-SQUARE_ON_SCALAR = (False, True, True, False)
+SQUARE_ON_SCALAR = (False, True, True, True)
 NORMS_AHEAD = False
 
 FLOPS = 2 * (2 * B * S + B) * K * D

@@ -19,7 +19,7 @@ CHUNKS = K // K_CHUNK
 PAIRS = S // 2
 UNITS = CHUNKS * PAIRS
 AHEAD = 2
-SQUARE_ON_SCALAR = (False, True, True, True)
+SQUARE_ON_SCALAR = (False, True, True, False)
 NORMS_AHEAD = False
 
 FLOPS = 2 * (2 * B * S + B) * K * D
@@ -34,7 +34,6 @@ def tile_mpl_kernel(tc, p, q, W, out):
         staging = ctx.enter_context(tc.tile_pool(name="staging", bufs=2))
         results = ctx.enter_context(tc.tile_pool(name="results", bufs=3))
         banks = ctx.enter_context(tc.psum_pool(name="banks", bufs=8))
-        ctx.enter_context(tc.manual_schedule())
 
         q_rows = inputs.tile([P, D], BF16, name="q_rows")
         p_rows = [inputs.tile([P, 2, D], BF16, name="p_rows%d" % pair) for pair in range(PAIRS)]

from contextlib import ExitStack

import concourse.mybir as mybir
from concourse.masks import make_identity

F32 = mybir.dt.float32
BF16 = mybir.dt.bfloat16
U32 = mybir.dt.uint32
U8 = mybir.dt.uint8
FP8X4 = mybir.dt.float8_e4m3fn_x4
ACT = mybir.ActivationFunctionType
ALU = mybir.AluOpType

P = 128
B, S, D, K = 128, 8, 1024, 2048
PASSES = D // (4 * P)
K_CHUNK = 256
CHUNKS = K // K_CHUNK
PAIRS = S // 2
UNITS = CHUNKS * PAIRS
AHEAD = 2
SQUARE_ON_SCALAR = (False, True, True, False)
NORMS_AHEAD = False

FLOPS = 2 * (2 * B * S + B) * K * D


def tile_mpl_kernel(tc, p, q, W, out):
    nc = tc.nc
    out_rows = out.rearrange("b s k -> b (s k)")
    with ExitStack() as ctx:
        inputs = ctx.enter_context(tc.tile_pool(name="inputs", bufs=1))
        operands = ctx.enter_context(tc.tile_pool(name="operands", bufs=1))
        staging = ctx.enter_context(tc.tile_pool(name="staging", bufs=2))
        results = ctx.enter_context(tc.tile_pool(name="results", bufs=3))
        banks = ctx.enter_context(tc.psum_pool(name="banks", bufs=8))

        q_rows = inputs.tile([P, D], BF16, name="q_rows")
        p_rows = [inputs.tile([P, 2, D], BF16, name="p_rows%d" % pair) for pair in range(PAIRS)]
        w_rows = [inputs.tile([P, 2, D], BF16, name="w_rows%d" % c) for c in range(CHUNKS)]

        def load_p(pair):
            nc.sync.dma_start(out=p_rows[pair][:], in_=p[:, 2 * pair : 2 * pair + 2, :])

        def load_w(c):
            rows = W[K_CHUNK * c : K_CHUNK * (c + 1), :]
            nc.sync.dma_start(out=w_rows[c][:], in_=rows.rearrange("(t r) d -> r t d", r=P))

        load_w(0)
        load_p(0)
        nc.sync.dma_start(out=q_rows[:], in_=q[:, S - 1, :])
        for pair in range(1, PAIRS):
            load_p(pair)
        for c in range(1, CHUNKS):
            load_w(c)

        identity = inputs.tile([P, P], F32, name="identity")
        make_identity(nc, identity[:])
        one = inputs.tile([P, 1], F32, name="one")
        nc.vector.memset(one[:], 1.0)
        warm = inputs.tile([P, 1], F32, name="warm")
        nc.scalar.activation(out=warm[:], in_=one[:], func=ACT.Abs_reciprocal_sqrt)

        q_flipped = inputs.tile([P, PASSES, 4 * P], BF16, name="q_flipped")
        qq_values = inputs.tile([P, PASSES * 4 * P], BF16, name="qq_values", align_bytes=64)
        qq_codes = operands.tile([P, PASSES * P], U32, name="qq_codes", align_bytes=64)
        qq_scales = operands.tile([P, PASSES * P], U8, name="qq_scales", align_bytes=64)
        pq_codes = [operands.tile([P, 512], U32, name="pq_codes%d" % i, align_bytes=64) for i in range(PAIRS)]
        pq_scales = [operands.tile([P, 512], U8, name="pq_scales%d" % i, align_bytes=64) for i in range(PAIRS)]
        pp_codes = [operands.tile([P, 512], U32, name="pp_codes%d" % i, align_bytes=64) for i in range(PAIRS)]
        pp_scales = [operands.tile([P, 512], U8, name="pp_scales%d" % i, align_bytes=64) for i in range(PAIRS)]
        w2_codes = [operands.tile([P, 512], U32, name="w2_codes%d" % c, align_bytes=64) for c in range(CHUNKS)]
        w2_scales = [operands.tile([P, 512], U8, name="w2_scales%d" % c, align_bytes=64) for c in range(CHUNKS)]
        q_factor = [operands.tile([P, K_CHUNK], F32, name="q_factor%d" % c) for c in range(CHUNKS)]
        live = {}

        def flip(rows, g):
            bank = banks.tile([P, 512], F32, name="bank")
            for u in range(2):
                for t in range(2):
                    nc.tensor.transpose(
                        out=bank[:, u * 256 + t * P : u * 256 + (t + 1) * P],
                        in_=rows[:, t, :].bitcast(F32)[:, 256 * g + P * u : 256 * g + P * (u + 1)],
                        identity=identity[:],
                    )
            return bank

        def copy_words(dst, bank):
            nc.scalar.copy(
                out=dst.bitcast(F32).rearrange("p (n u) -> p n u", u=2),
                in_=bank[:].rearrange("p (u n) -> p n u", u=2),
            )

        def square_words(dst, bank):
            nc.scalar.activation(
                out=dst.rearrange("p (n u e) -> p n u e", u=2, e=2),
                in_=bank[:].bitcast(BF16).rearrange("p (u n e) -> p n u e", u=2, e=2),
                func=ACT.Square,
            )

        def quantise(codes, scales, values):
            nc.vector.quantize_mx(out=codes[:].bitcast(FP8X4), scales=scales[:], in_=values)

        def q_flip():
            bank = banks.tile([P, 512], F32, name="bank")
            for u in range(2):
                for g in range(PASSES):
                    nc.tensor.transpose(
                        out=bank[:, u * 256 + g * P : u * 256 + (g + 1) * P],
                        in_=q_rows[:].bitcast(F32)[:, 256 * g + P * u : 256 * g + P * (u + 1)],
                        identity=identity[:],
                    )
            live["q"] = bank

        def p_flip(pair):
            for g in range(PASSES):
                live["p", pair, g] = flip(p_rows[pair], g)

        def p_copy(pair):
            if SQUARE_ON_SCALAR[pair]:
                return
            flipped = staging.tile([P, PASSES, 1024], BF16, name="p_flipped")
            live["p_flipped", pair] = flipped
            for g in range(PASSES):
                copy_words(flipped[:, g, :], live["p", pair, g])

        def p_square(pair):
            values = staging.tile([P, PASSES * 1024], BF16, name="pp_values", align_bytes=64)
            if SQUARE_ON_SCALAR[pair]:
                for g in range(PASSES):
                    square_words(values[:, g * 1024 : (g + 1) * 1024], live["p", pair, g])
            else:
                flat = live["p_flipped", pair][:].rearrange("p g n -> p (g n)")
                nc.vector.tensor_tensor(out=values[:], in0=flat, in1=flat, op=ALU.mult)
            quantise(pp_codes[pair], pp_scales[pair], values[:])

        def p_times_q(pair):
            values = staging.tile([P, PASSES, 1024], BF16, name="pq_values", align_bytes=64)
            for g in range(PASSES):
                if SQUARE_ON_SCALAR[pair]:
                    nc.vector.tensor_tensor(
                        out=values[:, g, :].rearrange("p (s n u e) -> p s n u e", s=2, u=2, e=2),
                        in0=live["p", pair, g][:].bitcast(BF16).rearrange("p (u s n e) -> p s n u e", u=2, s=2, e=2),
                        in1=q_flipped[:, g, :]
                        .rearrange("p (n u e) -> p n u e", u=2, e=2)
                        .unsqueeze(1)
                        .to_broadcast([P, 2, P, 2, 2]),
                        op=ALU.mult,
                    )
                else:
                    nc.vector.tensor_tensor(
                        out=values[:, g, :].rearrange("p (s n) -> p s n", s=2),
                        in0=live["p_flipped", pair][:, g, :].rearrange("p (s n) -> p s n", s=2),
                        in1=q_flipped[:, g, :].unsqueeze(1).to_broadcast([P, 2, 4 * P]),
                        op=ALU.mult,
                    )
            quantise(pq_codes[pair], pq_scales[pair], values[:].rearrange("p g n -> p (g n)"))

        def w_flip(c):
            for g in range(PASSES):
                live["w", c, g] = flip(w_rows[c], g)

        def w_square(c, g):
            if g == 0:
                live["w2", c] = staging.tile([P, PASSES, 1024], BF16, name="w2_values", align_bytes=64)
            values = live["w2", c]
            if c == 0:
                flipped = staging.tile([P, 1024], BF16, name="w_flipped")
                copy_words(flipped[:], live["w", c, g])
                nc.vector.tensor_tensor(out=values[:, g, :], in0=flipped[:], in1=flipped[:], op=ALU.mult)
            else:
                square_words(values[:, g, :], live["w", c, g])

        def w_quantise(c):
            quantise(w2_codes[c], w2_scales[c], live["w2", c][:].rearrange("p g n -> p (g n)"))

        def contract(sums, codes, scales, first, step, c):
            for g in range(PASSES):
                cols = slice((first + step * g) * P, (first + step * g + 1) * P)
                k_cols = slice(g * K_CHUNK, (g + 1) * K_CHUNK)
                nc.tensor.matmul_mx(
                    out=sums,
                    lhsT=codes[:, cols].bitcast(FP8X4),
                    lhsT_scale=scales[:, cols],
                    rhs=w2_codes[c][:, k_cols].bitcast(FP8X4),
                    rhs_scale=w2_scales[c][:, k_cols],
                    start=(g == 0),
                    stop=(g == PASSES - 1),
                )

        def q_norm(c):
            bank = banks.tile([P, 512], F32, name="bank")
            contract(bank[:, 0:K_CHUNK], qq_codes, qq_scales, 0, 1, c)
            nc.scalar.activation(
                out=q_factor[c][:], in_=bank[:, 0:K_CHUNK], func=ACT.Abs_reciprocal_sqrt, scale=float(D * D)
            )

        def p_norms(unit):
            c, pair = divmod(unit, PAIRS)
            bank = banks.tile([P, 512], F32, name="bank")
            for s in range(2):
                contract(bank[:, s * K_CHUNK : (s + 1) * K_CHUNK], pp_codes[pair], pp_scales[pair], s, 2, c)
            factor = results.tile([P, 2 * K_CHUNK], F32, name="p_factor")
            live["p_factor", unit] = factor
            nc.scalar.activation(
                out=factor[:].rearrange("p (k s) -> p k s", s=2),
                in_=bank[:].rearrange("p (s k) -> p k s", s=2),
                func=ACT.Abs_reciprocal_sqrt,
            )

        def dots(unit):
            c, pair = divmod(unit, PAIRS)
            bank = banks.tile([P, 512], F32, name="bank")
            for s in range(2):
                contract(bank[:, s * K_CHUNK : (s + 1) * K_CHUNK], pq_codes[pair], pq_scales[pair], s, 2, c)
            if pair == 0:
                live["cosines", c] = results.tile([P, PAIRS, 2 * K_CHUNK], F32, name="cosines")
            nc.vector.scalar_tensor_tensor(
                out=live["cosines", c][:, pair, :].rearrange("p (k s) -> p k s", s=2),
                in0=bank[:].rearrange("p (s k) -> p k s", s=2),
                scalar=-1.0,
                in1=live["p_factor", unit][:].rearrange("p (k s) -> p k s", s=2),
                op0=ALU.mult,
                op1=ALU.mult,
            )

        def finish(c, lo, hi):
            dist = results.tile([P, K_CHUNK * S], F32, name="dist")
            nc.vector.tensor_tensor(
                out=dist[:, 0 : (hi - lo) * S].rearrange("p (k a s) -> p k a s", a=PAIRS, s=2),
                in0=live["cosines", c][:].rearrange("p a (k s) -> p k a s", s=2)[:, lo:hi, :, :],
                in1=q_factor[c][:, lo:hi].unsqueeze(2).unsqueeze(3).to_broadcast([P, hi - lo, PAIRS, 2]),
                op=ALU.mult,
            )
            nc.sync.dma_start(
                out=out_rows[:, (c * K_CHUNK + lo) * S : (c * K_CHUNK + hi) * S], in_=dist[:, 0 : (hi - lo) * S]
            )

        w_flip(0)
        p_flip(0)
        q_flip()
        w_square(0, 0)
        w_square(0, 1)
        p_copy(0)
        square_words(qq_values[:], live["q"])
        copy_words(q_flipped[:].rearrange("p g n -> p (g n)"), live["q"])
        w_quantise(0)
        for pair in range(PAIRS):
            if pair > 0:
                p_copy(pair)
            if pair + 1 < PAIRS:
                p_flip(pair + 1)
            p_square(pair)
            if pair == 0:
                quantise(qq_codes, qq_scales, qq_values[:])
            p_times_q(pair)
        q_norm(0)
        w_flip(1)
        w_square(1, 0)
        w_square(1, 1)
        w_quantise(1)

        if NORMS_AHEAD:
            p_norms(0)
        for unit in range(UNITS):
            c, pair = divmod(unit, PAIRS)
            prepare = c + AHEAD < CHUNKS
            if pair == 0:
                if prepare:
                    w_flip(c + AHEAD)
                    w_square(c + AHEAD, 0)
                if c > 0:
                    q_norm(c)
            if pair == 1 and prepare:
                w_square(c + AHEAD, 1)
            if not NORMS_AHEAD:
                p_norms(unit)
            elif unit + 1 < UNITS:
                p_norms(unit + 1)
            dots(unit)
            if pair == 1 and prepare:
                w_quantise(c + AHEAD)
            if pair == PAIRS - 1:
                if c + 1 < CHUNKS:
                    finish(c, 0, K_CHUNK)
                else:
                    finish(c, 0, K_CHUNK // 2)
                    finish(c, K_CHUNK // 2, K_CHUNK)
